import numpy as np
import ml_dtypes

BF16 = ml_dtypes.bfloat16


def bf(x):
    return np.asarray(x, np.float32).astype(BF16)


def f32(x):
    return np.asarray(x, np.float32)


def f64(x):
    return np.asarray(x).astype(np.float64)


def striped(idx):
    return np.tile(idx.reshape(-1, 16).T, (8, 1))


C, S, KN, DK, NH, HP, RUNS, N = 512, 2048, 4, 32, 16, 1024, 8, 8192


def setup_inputs():
    return {
        "h": f32(np.random.standard_normal((C, S))),
        "wq": bf(np.random.standard_normal((C, C)) / np.sqrt(C)),
        "bq": f32(0.1 * np.random.standard_normal((C, 1))),
        "wkv": bf(np.random.standard_normal((C, C + C)) / np.sqrt(C)),
        "bv": f32(0.1 * np.random.standard_normal((C, 1))),
        "wo": bf(np.random.standard_normal((C, C)) / np.sqrt(C)),
        "bo": f32(0.1 * np.random.standard_normal((C, 1))),
        "offs": striped(np.concatenate([np.random.permutation(S)[:HP] for _ in range(RUNS)])),
    }


def reference(h, wq, bq, wkv, bv, wo, bo, offs):
    idx = offs[:16].T.reshape(-1)
    hh = f64(h)
    q = f64(wq).T @ hh + f64(bq)
    kv = f64(wkv).T @ hh
    kv[C:] += f64(bv)
    t = kv[:C][:, idx] * np.tile(q, (1, KN))
    sc = t.reshape(NH, DK, KN, S).sum(axis=1) / np.sqrt(DK)
    e = np.exp(sc - sc.max(axis=1, keepdims=True))
    p = e / e.sum(axis=1, keepdims=True)
    pb = np.repeat(p, DK, axis=0).reshape(C, N)
    u = kv[C:][:, idx] * pb
    ctx = u.reshape(C, KN, S).sum(axis=1)
    return f64(wo).T @ ctx + f64(bo)

@@ -1,0 +1,220 @@
+import math
+
+import concourse.mybir as mybir
+
+F32 = mybir.dt.float32
+BF16 = mybir.dt.bfloat16
+U16 = mybir.dt.uint16
+ALU = mybir.AluOpType
+FUNC = mybir.ActivationFunctionType
+
+P = 128
+C = 512
+CB = C // P
+S = 2048
+KN = 4
+DK = 32
+HB = P // DK
+N = KN * S
+BANK = 512
+NB = S // BANK
+PIECE = 1024
+W = 128
+GB = 2
+ROWS_OF_HEAD = S // W
+
+FLOPS = 2 * S * C * (4 * C) + 4 * C * N
+
+
+def tile_attentionfusion_b_kernel(tc, h, wq, bq, wkv, bv, wo, bo, offs, out):
+    nc = tc.nc
+    with (
+        tc.tile_pool(name="held", bufs=1) as held,
+        tc.psum_pool(name="psum", bufs=8) as psum,
+    ):
+        offsets = held.tile([P, N // 16], U16, name="offsets")
+        nc.sync.dma_start(offsets[:], offs)
+
+        wkv_sb = held.tile([P, CB, 2 * C], BF16, name="wkv_sb")
+        nc.scalar.dma_start(wkv_sb[:], wkv.rearrange("(i p) r -> p i r", p=P))
+        wq_sb = held.tile([P, CB, C], BF16, name="wq_sb")
+        nc.scalar.dma_start(wq_sb[:], wq.rearrange("(i p) c -> p i c", p=P))
+
+        h_bf = [held.tile([P, S], BF16, name=f"h_bf{i}") for i in range(CB)]
+        with tc.tile_pool(name="stage", bufs=CB) as stage:
+            for i in range(CB):
+                h_f32 = stage.tile([P, S], F32, name="h_f32")
+                nc.sync.dma_start(h_f32[:], h[i * P : (i + 1) * P, :])
+                nc.vector.tensor_copy(h_bf[i][:], h_f32[:])
+
+        wo_sb = held.tile([P, CB, C], BF16, name="wo_sb")
+        nc.scalar.dma_start(wo_sb[:], wo.rearrange("(i p) m -> p i m", p=P))
+        bq_sb = held.tile([P, CB], F32, name="bq_sb")
+        nc.scalar.dma_start(bq_sb[:], bq.rearrange("(b p) o -> p (b o)", p=P))
+        bv_sb = held.tile([P, CB], F32, name="bv_sb")
+        nc.scalar.dma_start(bv_sb[:], bv.rearrange("(b p) o -> p (b o)", p=P))
+        bo_sb = held.tile([P, CB], F32, name="bo_sb")
+        nc.scalar.dma_start(bo_sb[:], bo.rearrange("(b p) o -> p (b o)", p=P))
+
+        head_sum = held.tile([P, 2 * P], BF16, name="head_sum")
+        nc.vector.memset(head_sum[:], 0.0)
+        for hd in range(HB):
+            col = P + ROWS_OF_HEAD * hd
+            nc.vector.memset(head_sum[hd * DK : (hd + 1) * DK, col : col + 1], 1.0)
+
+        k_sb = [held.tile([P, S], F32, name=f"k_sb{b}") for b in range(CB)]
+        q_sb = [held.tile([P, S], F32, name=f"q_sb{b}") for b in range(CB)]
+        v_sb = [held.tile([P, S], F32, name=f"v_sb{b}") for b in range(CB)]
+        ctx_bf = [held.tile([P, S], BF16, name=f"ctx_bf{b}") for b in range(CB)]
+        out_last = held.tile([P, S], F32, name="out_last")
+
+        def parked(group):
+            rows = KN * GB * HB
+            first = C - (group + 1) * rows
+            return out[first : first + rows, :].rearrange("x n -> (x n)")
+
+        with (
+            tc.tile_pool(name="soft", bufs=1) as soft,
+            tc.tile_pool(name="t_ring", bufs=3) as t_ring,
+            tc.tile_pool(name="p_ring", bufs=3) as p_ring,
+            tc.tile_pool(name="u_ring", bufs=2) as u_ring,
+            tc.tile_pool(name="o_ring", bufs=2) as o_ring,
+        ):
+
+            def project(dst, w_sb, col0, bias):
+                for n in range(NB):
+                    cols = slice(n * BANK, (n + 1) * BANK)
+                    acc = psum.tile([P, BANK], F32, name="acc", tag="bank")
+                    for i in range(CB):
+                        nc.tensor.matmul(
+                            acc[:],
+                            w_sb[:, i, col0 : col0 + P],
+                            h_bf[i][:, cols],
+                            start=(i == 0),
+                            stop=(i == CB - 1),
+                        )
+                    if bias is None:
+                        nc.scalar.copy(dst[:, cols], acc[:])
+                    else:
+                        nc.scalar.activation(dst[:, cols], acc[:], FUNC.Identity, bias=bias)
+
+            def keys_times_queries(b, score):
+                for a in range(KN):
+                    for half in range(S // PIECE):
+                        j0 = a * S + half * PIECE
+                        t_f32 = t_ring.tile([P, PIECE], F32, name="t_f32")
+                        nc.vector.tensor_tensor(
+                            t_f32[:],
+                            k_sb[b][:].indirect(offsets[:, j0 // 16 : (j0 + PIECE) // 16]),
+                            q_sb[b][:, half * PIECE : (half + 1) * PIECE],
+                            ALU.mult,
+                        )
+                        t_bf = t_ring.tile([P, PIECE], BF16, name="t_bf")
+                        nc.scalar.copy(t_bf[:], t_f32[:])
+                        for x in range(PIECE // W):
+                            k = half * (PIECE // W) + x
+                            shift = (b % GB) * HB * ROWS_OF_HEAD + k
+                            nc.tensor.matmul(
+                                score[a][:, 0:W],
+                                head_sum[:, P - shift : 2 * P - shift],
+                                t_bf[:, x * W : (x + 1) * W],
+                                start=(b % GB == 0 and k == 0),
+                                stop=(b % GB == GB - 1 and k == ROWS_OF_HEAD - 1),
+                            )
+
+            def softmax(group, score):
+                sc = soft.tile([P, KN, W], F32, name="sc")
+                for a in range(KN):
+                    nc.scalar.mul(sc[:, a, :], score[a][:, 0:W], 1.0 / math.sqrt(DK))
+                max2 = soft.tile([P, 2, W], F32, name="max2")
+                nc.vector.tensor_max(max2[:], sc[:, 0:2, :], sc[:, 2:4, :])
+                max1 = soft.tile([P, W], F32, name="max1")
+                nc.vector.tensor_max(max1[:], max2[:, 0, :], max2[:, 1, :])
+                shifted = soft.tile([P, KN, W], F32, name="shifted")
+                nc.vector.tensor_sub(
+                    shifted[:], sc[:], max1[:].unsqueeze(1).to_broadcast([P, KN, W])
+                )
+                e = soft.tile([P, KN, W], F32, name="e")
+                nc.scalar.activation(e[:], shifted[:], FUNC.Exp)
+                sum2 = soft.tile([P, 2, W], F32, name="sum2")
+                nc.vector.tensor_add(sum2[:], e[:, 0:2, :], e[:, 2:4, :])
+                sum1 = soft.tile([P, W], F32, name="sum1")
+                nc.vector.tensor_add(sum1[:], sum2[:, 0, :], sum2[:, 1, :])
+                inv = soft.tile([P, W], F32, name="inv")
+                nc.vector.reciprocal(inv[:], sum1[:])
+                p = soft.tile([P, KN, W], F32, name="p")
+                nc.vector.tensor_mul(p[:], e[:], inv[:].unsqueeze(1).to_broadcast([P, KN, W]))
+                nc.sync.dma_start(
+                    parked(group).rearrange("(a r w) -> r a w", a=KN, w=W), p[:]
+                )
+
+            def attend(b, g):
+                by_head = parked(b // GB).rearrange("(a r n) -> r a n", a=KN, n=S)
+                p_full = p_ring.tile([P, KN, BANK], F32, name="p_full")
+                for hd in range(HB):
+                    one_head = by_head[(b % GB) * HB + hd, :, g * BANK : (g + 1) * BANK]
+                    nc.sync.dma_start(
+                        p_full[hd * DK : (hd + 1) * DK, :, :],
+                        one_head.unsqueeze(0).to_broadcast([DK, KN, BANK]),
+                    )
+                u = u_ring.tile([P, KN, BANK], F32, name="u")
+                for a in range(KN):
+                    j0 = a * S + g * BANK
+                    nc.vector.tensor_tensor(
+                        u[:, a, :],
+                        v_sb[b][:].indirect(offsets[:, j0 // 16 : (j0 + BANK) // 16]),
+                        p_full[:, a, :],
+                        ALU.mult,
+                    )
+                pair = u_ring.tile([P, 2, BANK], F32, name="pair")
+                nc.vector.tensor_add(pair[:], u[:, 0:2, :], u[:, 2:4, :])
+                nc.vector.tensor_add(
+                    ctx_bf[b][:, g * BANK : (g + 1) * BANK], pair[:, 0, :], pair[:, 1, :]
+                )
+
+            def project_out(g):
+                cols = slice(g * BANK, (g + 1) * BANK)
+                for m in range(CB):
+                    acc = psum.tile([P, BANK], F32, name="acc", tag="bank")
+                    for b in range(CB):
+                        nc.tensor.matmul(
+                            acc[:],
+                            wo_sb[:, b, m * P : (m + 1) * P],
+                            ctx_bf[b][:, cols],
+                            start=(b == 0),
+                            stop=(b == CB - 1),
+                        )
+                    if m < CB - 1:
+                        o = o_ring.tile([P, BANK], F32, name="o")
+                        nc.scalar.activation(o[:], acc[:], FUNC.Identity, bias=bo_sb[:, m : m + 1])
+                        nc.sync.dma_start(out[m * P : (m + 1) * P, cols], o[:])
+                    else:
+                        nc.scalar.activation(
+                            out_last[:, cols], acc[:], FUNC.Identity, bias=bo_sb[:, m : m + 1]
+                        )
+
+            project(k_sb[0], wkv_sb, 0, None)
+            project(q_sb[0], wq_sb, 0, bq_sb[:, 0:1])
+            score = []
+            for b in range(CB):
+                if b + 1 < CB:
+                    project(k_sb[b + 1], wkv_sb, (b + 1) * P, None)
+                    project(q_sb[b + 1], wq_sb, (b + 1) * P, bq_sb[:, b + 1 : b + 2])
+                if b % GB == 0:
+                    score = [
+                        psum.tile([P, BANK], F32, name=f"score{a}", tag="bank") for a in range(KN)
+                    ]
+                keys_times_queries(b, score)
+                project(v_sb[b], wkv_sb, C + b * P, bv_sb[:, b : b + 1])
+                if b % GB == GB - 1:
+                    softmax(b // GB, score)
+
+            for group in range(CB // GB):
+                for g in range(NB):
+                    for b in range(group * GB, (group + 1) * GB):
+                        attend(b, g)
+                    if group == CB // GB - 1:
+                        project_out(g)
+            for g in range(NB):
+                cols = slice(g * BANK, (g + 1) * BANK)
+                nc.sync.dma_start(out[(CB - 1) * P : CB * P, cols], out_last[:, cols])

@@ -1,6 +1,7 @@
 import math
 
 import concourse.mybir as mybir
+from concourse.masks import make_identity
 
 F32 = mybir.dt.float32
 BF16 = mybir.dt.bfloat16
@@ -19,9 +20,14 @@ N = KN * S
 BANK = 512
 NB = S // BANK
 PIECE = 1024
-W = 128
+PT = S // P
 GB = 2
-ROWS_OF_HEAD = S // W
+GH = GB * HB
+GROUPS = CB // GB
+KEY_ITEMS = CB * N // PIECE
+KEY_ITEMS_B = N // PIECE
+STEPS = CB * NB
+AHEAD = 3
 
 FLOPS = 2 * S * C * (4 * C) + 4 * C * N
 
@@ -30,191 +36,260 @@ def tile_attentionfusion_b_kernel(tc, h, wq, bq, wkv, bv, wo, bo, offs, out):
     nc = tc.nc
     with (
         tc.tile_pool(name="held", bufs=1) as held,
+        tc.tile_pool(name="soft", bufs=1) as soft,
         tc.psum_pool(name="psum", bufs=8) as psum,
     ):
         offsets = held.tile([P, N // 16], U16, name="offsets")
         nc.sync.dma_start(offsets[:], offs)
 
-        wkv_sb = held.tile([P, CB, 2 * C], BF16, name="wkv_sb")
-        nc.scalar.dma_start(wkv_sb[:], wkv.rearrange("(i p) r -> p i r", p=P))
-        wq_sb = held.tile([P, CB, C], BF16, name="wq_sb")
-        nc.scalar.dma_start(wq_sb[:], wq.rearrange("(i p) c -> p i c", p=P))
-
-        h_bf = [held.tile([P, S], BF16, name=f"h_bf{i}") for i in range(CB)]
-        with tc.tile_pool(name="stage", bufs=CB) as stage:
-            for i in range(CB):
-                h_f32 = stage.tile([P, S], F32, name="h_f32")
-                nc.sync.dma_start(h_f32[:], h[i * P : (i + 1) * P, :])
-                nc.vector.tensor_copy(h_bf[i][:], h_f32[:])
-
-        wo_sb = held.tile([P, CB, C], BF16, name="wo_sb")
-        nc.scalar.dma_start(wo_sb[:], wo.rearrange("(i p) m -> p i m", p=P))
         bq_sb = held.tile([P, CB], F32, name="bq_sb")
         nc.scalar.dma_start(bq_sb[:], bq.rearrange("(b p) o -> p (b o)", p=P))
+        wk_sb = held.tile([P, CB, C], BF16, name="wk_sb")
+        nc.scalar.dma_start(wk_sb[:], wkv[:, 0:C].rearrange("(i p) r -> p i r", p=P))
+        wq_sb = held.tile([P, CB, C], BF16, name="wq_sb")
+        nc.scalar.dma_start(wq_sb[:], wq.rearrange("(i p) c -> p i c", p=P))
+        wv_sb = held.tile([P, CB, C], BF16, name="wv_sb")
         bv_sb = held.tile([P, CB], F32, name="bv_sb")
-        nc.scalar.dma_start(bv_sb[:], bv.rearrange("(b p) o -> p (b o)", p=P))
+        wo_sb = held.tile([P, CB, C], BF16, name="wo_sb")
         bo_sb = held.tile([P, CB], F32, name="bo_sb")
-        nc.scalar.dma_start(bo_sb[:], bo.rearrange("(b p) o -> p (b o)", p=P))
 
-        head_sum = held.tile([P, 2 * P], BF16, name="head_sum")
-        nc.vector.memset(head_sum[:], 0.0)
+        head_sel = held.tile([P, HB], BF16, name="head_sel")
+        nc.vector.memset(head_sel[:], 0.0)
         for hd in range(HB):
-            col = P + ROWS_OF_HEAD * hd
-            nc.vector.memset(head_sum[hd * DK : (hd + 1) * DK, col : col + 1], 1.0)
+            nc.vector.memset(head_sel[hd * DK : (hd + 1) * DK, hd : hd + 1], 1.0)
+        ident = held.tile([P, P], F32, name="ident")
+        make_identity(nc, ident[:])
+        ident_bf = held.tile([P, P], BF16, name="ident_bf")
+        make_identity(nc, ident_bf[:])
 
+        h_bf = [held.tile([P, CB, BANK], BF16, name=f"h_bf{n}") for n in range(NB)]
         k_sb = [held.tile([P, S], F32, name=f"k_sb{b}") for b in range(CB)]
         q_sb = [held.tile([P, S], F32, name=f"q_sb{b}") for b in range(CB)]
         v_sb = [held.tile([P, S], F32, name=f"v_sb{b}") for b in range(CB)]
         ctx_bf = [held.tile([P, S], BF16, name=f"ctx_bf{b}") for b in range(CB)]
         out_last = held.tile([P, S], F32, name="out_last")
 
+        def project_chunk(dst, w_sb, bias, b, n):
+            acc = psum.tile([P, BANK], F32, name="acc", tag="bank")
+            for i in range(CB):
+                nc.tensor.matmul(
+                    acc[:],
+                    w_sb[:, i, b * P : (b + 1) * P],
+                    h_bf[n][:, i, :],
+                    start=(i == 0),
+                    stop=(i == CB - 1),
+                )
+            cols = slice(n * BANK, (n + 1) * BANK)
+            if bias is None:
+                nc.scalar.copy(dst[:, cols], acc[:])
+            else:
+                nc.scalar.activation(dst[:, cols], acc[:], FUNC.Identity, bias=bias[:, b : b + 1])
+
         def parked(group):
-            rows = KN * GB * HB
+            rows = KN * GH
             first = C - (group + 1) * rows
             return out[first : first + rows, :].rearrange("x n -> (x n)")
 
-        with (
-            tc.tile_pool(name="soft", bufs=1) as soft,
-            tc.tile_pool(name="t_ring", bufs=3) as t_ring,
-            tc.tile_pool(name="p_ring", bufs=3) as p_ring,
-            tc.tile_pool(name="u_ring", bufs=2) as u_ring,
-            tc.tile_pool(name="o_ring", bufs=2) as o_ring,
-        ):
-
-            def project(dst, w_sb, col0, bias):
-                for n in range(NB):
-                    cols = slice(n * BANK, (n + 1) * BANK)
-                    acc = psum.tile([P, BANK], F32, name="acc", tag="bank")
-                    for i in range(CB):
-                        nc.tensor.matmul(
-                            acc[:],
-                            w_sb[:, i, col0 : col0 + P],
-                            h_bf[i][:, cols],
-                            start=(i == 0),
-                            stop=(i == CB - 1),
-                        )
-                    if bias is None:
-                        nc.scalar.copy(dst[:, cols], acc[:])
-                    else:
-                        nc.scalar.activation(dst[:, cols], acc[:], FUNC.Identity, bias=bias)
-
-            def keys_times_queries(b, score):
-                for a in range(KN):
-                    for half in range(S // PIECE):
-                        j0 = a * S + half * PIECE
-                        t_f32 = t_ring.tile([P, PIECE], F32, name="t_f32")
-                        nc.vector.tensor_tensor(
-                            t_f32[:],
-                            k_sb[b][:].indirect(offsets[:, j0 // 16 : (j0 + PIECE) // 16]),
-                            q_sb[b][:, half * PIECE : (half + 1) * PIECE],
-                            ALU.mult,
-                        )
-                        t_bf = t_ring.tile([P, PIECE], BF16, name="t_bf")
-                        nc.scalar.copy(t_bf[:], t_f32[:])
-                        for x in range(PIECE // W):
-                            k = half * (PIECE // W) + x
-                            shift = (b % GB) * HB * ROWS_OF_HEAD + k
-                            nc.tensor.matmul(
-                                score[a][:, 0:W],
-                                head_sum[:, P - shift : 2 * P - shift],
-                                t_bf[:, x * W : (x + 1) * W],
-                                start=(b % GB == 0 and k == 0),
-                                stop=(b % GB == GB - 1 and k == ROWS_OF_HEAD - 1),
-                            )
-
-            def softmax(group, score):
-                sc = soft.tile([P, KN, W], F32, name="sc")
-                for a in range(KN):
-                    nc.scalar.mul(sc[:, a, :], score[a][:, 0:W], 1.0 / math.sqrt(DK))
-                max2 = soft.tile([P, 2, W], F32, name="max2")
-                nc.vector.tensor_max(max2[:], sc[:, 0:2, :], sc[:, 2:4, :])
-                max1 = soft.tile([P, W], F32, name="max1")
-                nc.vector.tensor_max(max1[:], max2[:, 0, :], max2[:, 1, :])
-                shifted = soft.tile([P, KN, W], F32, name="shifted")
-                nc.vector.tensor_sub(
-                    shifted[:], sc[:], max1[:].unsqueeze(1).to_broadcast([P, KN, W])
-                )
-                e = soft.tile([P, KN, W], F32, name="e")
-                nc.scalar.activation(e[:], shifted[:], FUNC.Exp)
-                sum2 = soft.tile([P, 2, W], F32, name="sum2")
-                nc.vector.tensor_add(sum2[:], e[:, 0:2, :], e[:, 2:4, :])
-                sum1 = soft.tile([P, W], F32, name="sum1")
-                nc.vector.tensor_add(sum1[:], sum2[:, 0, :], sum2[:, 1, :])
-                inv = soft.tile([P, W], F32, name="inv")
-                nc.vector.reciprocal(inv[:], sum1[:])
-                p = soft.tile([P, KN, W], F32, name="p")
-                nc.vector.tensor_mul(p[:], e[:], inv[:].unsqueeze(1).to_broadcast([P, KN, W]))
+        with tc.tile_pool(name="stage", bufs=NB) as stage:
+            h_f32 = [stage.tile([P, CB, BANK], F32, name="h_f32") for n in range(NB)]
+            for n in range(NB):
                 nc.sync.dma_start(
-                    parked(group).rearrange("(a r w) -> r a w", a=KN, w=W), p[:]
+                    h_f32[n][:], h[:, n * BANK : (n + 1) * BANK].rearrange("(i p) n -> p i n", p=P)
+                )
+            nc.sync.dma_start(wv_sb[:], wkv[:, C : 2 * C].rearrange("(i p) r -> p i r", p=P))
+            nc.sync.dma_start(bv_sb[:], bv.rearrange("(b p) o -> p (b o)", p=P))
+            nc.sync.dma_start(wo_sb[:], wo.rearrange("(i p) m -> p i m", p=P))
+            nc.sync.dma_start(bo_sb[:], bo.rearrange("(b p) o -> p (b o)", p=P))
+            for n in range(NB):
+                nc.vector.tensor_copy(h_bf[n][:], h_f32[n][:])
+                project_chunk(k_sb[0], wk_sb, None, 0, n)
+                project_chunk(q_sb[0], wq_sb, bq_sb, 0, n)
+
+        scores = []
+        soft_tiles = []
+
+        def softmax_stage(group, stage):
+            if stage == 0:
+                soft_tiles.append(
+                    {
+                        "sc": soft.tile([P, KN, P], F32, name="sc"),
+                        "max2": soft.tile([P, 2, P], F32, name="max2"),
+                        "max1": soft.tile([P, P], F32, name="max1"),
+                        "e": soft.tile([P, KN, P], F32, name="e"),
+                        "sum2": soft.tile([P, 2, P], F32, name="sum2"),
+                        "sum1": soft.tile([P, P], F32, name="sum1"),
+                        "inv": soft.tile([P, P], F32, name="inv"),
+                        "p": soft.tile([P, KN, P], F32, name="p"),
+                        "p_rows": soft.tile([P, KN, P], F32, name="p_rows"),
+                    }
+                )
+            t = soft_tiles[group]
+            over_slots = [P, KN, P]
+            if stage == 0:
+                nc.scalar.mul(t["sc"][:], scores[group][:], 1.0 / math.sqrt(DK))
+            if stage == 1:
+                nc.vector.tensor_max(t["max2"][:], t["sc"][:, 0:2, :], t["sc"][:, 2:4, :])
+                nc.vector.tensor_max(t["max1"][:], t["max2"][:, 0, :], t["max2"][:, 1, :])
+                nc.vector.tensor_sub(
+                    t["sc"][:], t["sc"][:], t["max1"][:].unsqueeze(1).to_broadcast(over_slots)
+                )
+                nc.scalar.activation(t["e"][:], t["sc"][:], FUNC.Exp)
+            if stage == 2:
+                nc.vector.tensor_add(t["sum2"][:], t["e"][:, 0:2, :], t["e"][:, 2:4, :])
+                nc.vector.tensor_add(t["sum1"][:], t["sum2"][:, 0, :], t["sum2"][:, 1, :])
+                nc.vector.reciprocal(t["inv"][:], t["sum1"][:])
+                nc.vector.tensor_mul(
+                    t["p"][:], t["e"][:], t["inv"][:].unsqueeze(1).to_broadcast(over_slots)
+                )
+                flipped = psum.tile([P, KN, P], F32, name="flipped", tag="bank")
+                for a in range(KN):
+                    nc.tensor.transpose(flipped[:, a, :], t["p"][:, a, :], ident[:])
+                nc.scalar.copy(t["p_rows"][:], flipped[:])
+                nc.sync.dma_start(
+                    parked(group).rearrange("(a r w) -> r a w", a=KN, w=P), t["p_rows"][:]
                 )
 
-            def attend(b, g):
+        def softmax_after(item):
+            for group in range(GROUPS):
+                stage = item - (group + 1) * GB * KEY_ITEMS_B
+                if 0 <= stage < 3:
+                    softmax_stage(group, stage)
+
+        def head_sums(t_bf, b, a, half):
+            by_head = scores[b // GB][:].rearrange("p a (r k) -> p a r k", k=PT)
+            for x in range(PIECE // P):
+                nc.tensor.matmul(
+                    by_head[:, a, (b % GB) * HB : (b % GB + 1) * HB, half * (PIECE // P) + x],
+                    t_bf[:, x * P : (x + 1) * P],
+                    head_sel[:],
+                    start=True,
+                    stop=True,
+                )
+
+        with (
+            tc.tile_pool(name="p_ring", bufs=AHEAD) as p_ring,
+            tc.tile_pool(name="u_ring", bufs=3) as u_ring,
+        ):
+            p_full = {}
+
+            def block_and_chunk(step):
+                group, rest = divmod(step, GB * NB)
+                g, x = divmod(rest, GB)
+                return group * GB + x, g
+
+            def fetch_p(step):
+                b, g = block_and_chunk(step)
                 by_head = parked(b // GB).rearrange("(a r n) -> r a n", a=KN, n=S)
-                p_full = p_ring.tile([P, KN, BANK], F32, name="p_full")
+                p_full[step] = p_ring.tile([P, KN, BANK], F32, name="p_full")
                 for hd in range(HB):
                     one_head = by_head[(b % GB) * HB + hd, :, g * BANK : (g + 1) * BANK]
                     nc.sync.dma_start(
-                        p_full[hd * DK : (hd + 1) * DK, :, :],
+                        p_full[step][hd * DK : (hd + 1) * DK, :, :],
                         one_head.unsqueeze(0).to_broadcast([DK, KN, BANK]),
                     )
-                u = u_ring.tile([P, KN, BANK], F32, name="u")
-                for a in range(KN):
-                    j0 = a * S + g * BANK
+
+            with tc.tile_pool(name="t_ring", bufs=3) as t_ring:
+                before = None
+                for item in range(KEY_ITEMS):
+                    b, rest = divmod(item, KEY_ITEMS_B)
+                    a, half = divmod(rest, S // PIECE)
+                    if item % (GB * KEY_ITEMS_B) == 0:
+                        scores.append(psum.tile([P, KN, P], F32, name="score", tag="bank"))
+                    j0 = a * S + half * PIECE
+                    t_f32 = t_ring.tile([P, PIECE], F32, name="t_f32")
                     nc.vector.tensor_tensor(
-                        u[:, a, :],
-                        v_sb[b][:].indirect(offsets[:, j0 // 16 : (j0 + BANK) // 16]),
-                        p_full[:, a, :],
+                        t_f32[:],
+                        k_sb[b][:].indirect(offsets[:, j0 // 16 : (j0 + PIECE) // 16]),
+                        q_sb[b][:, half * PIECE : (half + 1) * PIECE],
                         ALU.mult,
                     )
-                pair = u_ring.tile([P, 2, BANK], F32, name="pair")
-                nc.vector.tensor_add(pair[:], u[:, 0:2, :], u[:, 2:4, :])
-                nc.vector.tensor_add(
-                    ctx_bf[b][:, g * BANK : (g + 1) * BANK], pair[:, 0, :], pair[:, 1, :]
-                )
+                    t_bf = t_ring.tile([P, PIECE], BF16, name="t_bf")
+                    nc.scalar.copy(t_bf[:], t_f32[:])
+                    if b + 1 < CB:
+                        if rest < NB:
+                            project_chunk(k_sb[b + 1], wk_sb, None, b + 1, rest)
+                        else:
+                            project_chunk(q_sb[b + 1], wq_sb, bq_sb, b + 1, rest - NB)
+                    if item % 2 == 0:
+                        project_chunk(v_sb[item // 2 // NB], wv_sb, bv_sb, item // 2 // NB, item // 2 % NB)
+                    if before is not None:
+                        head_sums(*before)
+                    before = (t_bf, b, a, half)
+                    softmax_after(item)
+                    if item == GB * KEY_ITEMS_B + 2:
+                        for step in range(AHEAD):
+                            fetch_p(step)
+                head_sums(*before)
+                softmax_after(KEY_ITEMS)
 
-            def project_out(g):
-                cols = slice(g * BANK, (g + 1) * BANK)
-                for m in range(CB):
-                    acc = psum.tile([P, BANK], F32, name="acc", tag="bank")
-                    for b in range(CB):
-                        nc.tensor.matmul(
-                            acc[:],
-                            wo_sb[:, b, m * P : (m + 1) * P],
-                            ctx_bf[b][:, cols],
-                            start=(b == 0),
-                            stop=(b == CB - 1),
+            with tc.tile_pool(name="o_ring", bufs=2) as o_ring:
+                out_acc = []
+
+                def add_to_out(g, blocks):
+                    for x in blocks:
+                        for m in range(CB):
+                            nc.tensor.matmul(
+                                out_acc[m][:],
+                                wo_sb[:, x, m * P : (m + 1) * P],
+                                ctx_bf[x][:, g * BANK : (g + 1) * BANK],
+                                start=(x == 0),
+                                stop=(x == CB - 1),
+                            )
+
+                for step in range(STEPS):
+                    b, g = block_and_chunk(step)
+                    cols = slice(g * BANK, (g + 1) * BANK)
+                    last_group = b // GB == GROUPS - 1
+                    if last_group and b % GB == 0:
+                        out_acc.clear()
+                        out_acc.extend(
+                            psum.tile([P, BANK], F32, name=f"out_acc{m}", tag="bank") for m in range(CB)
                         )
-                    if m < CB - 1:
-                        o = o_ring.tile([P, BANK], F32, name="o")
-                        nc.scalar.activation(o[:], acc[:], FUNC.Identity, bias=bo_sb[:, m : m + 1])
-                        nc.sync.dma_start(out[m * P : (m + 1) * P, cols], o[:])
-                    else:
-                        nc.scalar.activation(
-                            out_last[:, cols], acc[:], FUNC.Identity, bias=bo_sb[:, m : m + 1]
+                        add_to_out(g, range(GB))
+
+                    u = u_ring.tile([P, KN, BANK], F32, name="u")
+                    for a in range(KN):
+                        j0 = a * S + g * BANK
+                        nc.vector.tensor_tensor(
+                            u[:, a, :],
+                            v_sb[b][:].indirect(offsets[:, j0 // 16 : (j0 + BANK) // 16]),
+                            p_full[step][:, a, :],
+                            ALU.mult,
                         )
+                    ctx_t = psum.tile([P, BANK // P, P], F32, name="ctx_t", tag="bank")
+                    for x in range(BANK // P):
+                        for a in range(KN):
+                            nc.tensor.matmul(
+                                ctx_t[:, x, :],
+                                u[:, a, x * P : (x + 1) * P],
+                                ident[:],
+                                start=(a == 0),
+                                stop=(a == KN - 1),
+                                is_transpose=True,
+                            )
+                    ctx_t_bf = o_ring.tile([P, BANK // P, P], BF16, name="ctx_t_bf")
+                    nc.scalar.copy(ctx_t_bf[:], ctx_t[:])
+                    ctx_ps = psum.tile([P, BANK], BF16, name="ctx_ps", tag="bank")
+                    for x in range(BANK // P):
+                        nc.tensor.transpose(ctx_ps[:, x * P : (x + 1) * P], ctx_t_bf[:, x, :], ident_bf[:])
+                    nc.scalar.copy(ctx_bf[b][:, cols], ctx_ps[:])
+                    if step + AHEAD < STEPS:
+                        fetch_p(step + AHEAD)
+                    softmax_after(KEY_ITEMS + 1 + step)
 
-            project(k_sb[0], wkv_sb, 0, None)
-            project(q_sb[0], wq_sb, 0, bq_sb[:, 0:1])
-            score = []
-            for b in range(CB):
-                if b + 1 < CB:
-                    project(k_sb[b + 1], wkv_sb, (b + 1) * P, None)
-                    project(q_sb[b + 1], wq_sb, (b + 1) * P, bq_sb[:, b + 1 : b + 2])
-                if b % GB == 0:
-                    score = [
-                        psum.tile([P, BANK], F32, name=f"score{a}", tag="bank") for a in range(KN)
-                    ]
-                keys_times_queries(b, score)
-                project(v_sb[b], wkv_sb, C + b * P, bv_sb[:, b : b + 1])
-                if b % GB == GB - 1:
-                    softmax(b // GB, score)
-
-            for group in range(CB // GB):
+                    if last_group and b % GB == GB - 1:
+                        add_to_out(g, range(GB, CB))
+                        for m in range(CB):
+                            if m < CB - 1:
+                                o = o_ring.tile([P, BANK], F32, name="o")
+                                nc.scalar.activation(
+                                    o[:], out_acc[m][:], FUNC.Identity, bias=bo_sb[:, m : m + 1]
+                                )
+                                nc.sync.dma_start(out[m * P : (m + 1) * P, cols], o[:])
+                            else:
+                                nc.scalar.activation(
+                                    out_last[:, cols], out_acc[m][:], FUNC.Identity, bias=bo_sb[:, m : m + 1]
+                                )
                 for g in range(NB):
-                    for b in range(group * GB, (group + 1) * GB):
-                        attend(b, g)
-                    if group == CB // GB - 1:
-                        project_out(g)
-            for g in range(NB):
-                cols = slice(g * BANK, (g + 1) * BANK)
-                nc.sync.dma_start(out[(CB - 1) * P : CB * P, cols], out_last[:, cols])
+                    cols = slice(g * BANK, (g + 1) * BANK)
+                    nc.sync.dma_start(out[(CB - 1) * P : CB * P, cols], out_last[:, cols])

@@ -19,15 +19,14 @@ HB = P // DK
 N = KN * S
 BANK = 512
 NB = S // BANK
-PIECE = 1024
 PT = S // P
 GB = 2
 GH = GB * HB
 GROUPS = CB // GB
-KEY_ITEMS = CB * N // PIECE
-KEY_ITEMS_B = N // PIECE
-STEPS = CB * NB
+KEY_ITEMS = CB * KN
+WIDE = 1024
 AHEAD = 3
+SOFTMAX_LAG = (0, 2, 3)
 
 FLOPS = 2 * S * C * (4 * C) + 4 * C * N
 
@@ -37,6 +36,7 @@ def tile_attentionfusion_b_kernel(tc, h, wq, bq, wkv, bv, wo, bo, offs, out):
     with (
         tc.tile_pool(name="held", bufs=1) as held,
         tc.tile_pool(name="soft", bufs=1) as soft,
+        tc.tile_pool(name="kq_ring", bufs=2) as kq_ring,
         tc.psum_pool(name="psum", bufs=8) as psum,
     ):
         offsets = held.tile([P, N // 16], U16, name="offsets")
@@ -63,11 +63,10 @@ def tile_attentionfusion_b_kernel(tc, h, wq, bq, wkv, bv, wo, bo, offs, out):
         make_identity(nc, ident_bf[:])
 
         h_bf = [held.tile([P, CB, BANK], BF16, name=f"h_bf{n}") for n in range(NB)]
-        k_sb = [held.tile([P, S], F32, name=f"k_sb{b}") for b in range(CB)]
-        q_sb = [held.tile([P, S], F32, name=f"q_sb{b}") for b in range(CB)]
+        k_sb = {}
+        q_sb = {}
         v_sb = [held.tile([P, S], F32, name=f"v_sb{b}") for b in range(CB)]
         ctx_bf = [held.tile([P, S], BF16, name=f"ctx_bf{b}") for b in range(CB)]
-        out_last = held.tile([P, S], F32, name="out_last")
 
         def project_chunk(dst, w_sb, bias, b, n):
             acc = psum.tile([P, BANK], F32, name="acc", tag="bank")
@@ -100,6 +99,8 @@ def tile_attentionfusion_b_kernel(tc, h, wq, bq, wkv, bv, wo, bo, offs, out):
             nc.sync.dma_start(bv_sb[:], bv.rearrange("(b p) o -> p (b o)", p=P))
             nc.sync.dma_start(wo_sb[:], wo.rearrange("(i p) m -> p i m", p=P))
             nc.sync.dma_start(bo_sb[:], bo.rearrange("(b p) o -> p (b o)", p=P))
+            k_sb[0] = kq_ring.tile([P, S], F32, name="k_sb")
+            q_sb[0] = kq_ring.tile([P, S], F32, name="q_sb")
             for n in range(NB):
                 nc.vector.tensor_copy(h_bf[n][:], h_f32[n][:])
                 project_chunk(k_sb[0], wk_sb, None, 0, n)
@@ -151,145 +152,145 @@ def tile_attentionfusion_b_kernel(tc, h, wq, bq, wkv, bv, wo, bo, offs, out):
 
         def softmax_after(item):
             for group in range(GROUPS):
-                stage = item - (group + 1) * GB * KEY_ITEMS_B
-                if 0 <= stage < 3:
-                    softmax_stage(group, stage)
+                lag = item - (group + 1) * GB * KN
+                if lag in SOFTMAX_LAG:
+                    softmax_stage(group, SOFTMAX_LAG.index(lag))
+                    if lag == SOFTMAX_LAG[-1]:
+                        for step in range(AHEAD):
+                            if steps[step][0] // GB == group:
+                                fetch_p(step)
 
-        def head_sums(t_bf, b, a, half):
+        def head_sums(t_bf, b, a):
             by_head = scores[b // GB][:].rearrange("p a (r k) -> p a r k", k=PT)
-            for x in range(PIECE // P):
+            for k in range(PT):
                 nc.tensor.matmul(
-                    by_head[:, a, (b % GB) * HB : (b % GB + 1) * HB, half * (PIECE // P) + x],
-                    t_bf[:, x * P : (x + 1) * P],
+                    by_head[:, a, (b % GB) * HB : (b % GB + 1) * HB, k],
+                    t_bf[:, k * P : (k + 1) * P],
                     head_sel[:],
                     start=True,
                     stop=True,
                 )
 
+        steps = []
+        for n0 in range(0, S, WIDE):
+            steps.extend((b, n0, WIDE) for b in range(CB - 1))
+            steps.extend((CB - 1, n0 + x, BANK) for x in range(0, WIDE, BANK))
+
         with (
             tc.tile_pool(name="p_ring", bufs=AHEAD) as p_ring,
-            tc.tile_pool(name="u_ring", bufs=3) as u_ring,
+            tc.tile_pool(name="u_ring", bufs=2) as u_ring,
         ):
             p_full = {}
 
-            def block_and_chunk(step):
-                group, rest = divmod(step, GB * NB)
-                g, x = divmod(rest, GB)
-                return group * GB + x, g
-
             def fetch_p(step):
-                b, g = block_and_chunk(step)
+                b, n0, width = steps[step]
                 by_head = parked(b // GB).rearrange("(a r n) -> r a n", a=KN, n=S)
-                p_full[step] = p_ring.tile([P, KN, BANK], F32, name="p_full")
+                p_full[step] = p_ring.tile([P, KN, WIDE], F32, name="p_full")
                 for hd in range(HB):
-                    one_head = by_head[(b % GB) * HB + hd, :, g * BANK : (g + 1) * BANK]
                     nc.sync.dma_start(
-                        p_full[step][hd * DK : (hd + 1) * DK, :, :],
-                        one_head.unsqueeze(0).to_broadcast([DK, KN, BANK]),
+                        p_full[step][hd * DK : (hd + 1) * DK, :, 0:width],
+                        by_head[(b % GB) * HB + hd, :, n0 : n0 + width]
+                        .unsqueeze(0)
+                        .to_broadcast([DK, KN, width]),
                     )
 
-            with tc.tile_pool(name="t_ring", bufs=3) as t_ring:
+            with tc.tile_pool(name="t_ring", bufs=2) as t_ring:
                 before = None
                 for item in range(KEY_ITEMS):
-                    b, rest = divmod(item, KEY_ITEMS_B)
-                    a, half = divmod(rest, S // PIECE)
-                    if item % (GB * KEY_ITEMS_B) == 0:
+                    b, a = divmod(item, KN)
+                    if item % (GB * KN) == 0:
                         scores.append(psum.tile([P, KN, P], F32, name="score", tag="bank"))
-                    j0 = a * S + half * PIECE
-                    t_f32 = t_ring.tile([P, PIECE], F32, name="t_f32")
+                    if b + 1 < CB:
+                        if a == 0:
+                            k_sb[b + 1] = kq_ring.tile([P, S], F32, name="k_sb")
+                            q_sb[b + 1] = kq_ring.tile([P, S], F32, name="q_sb")
+                        for n in (2 * a % NB, 2 * a % NB + 1):
+                            if a < KN // 2:
+                                project_chunk(k_sb[b + 1], wk_sb, None, b + 1, n)
+                            else:
+                                project_chunk(q_sb[b + 1], wq_sb, bq_sb, b + 1, n)
+                    project_chunk(v_sb[item // NB], wv_sb, bv_sb, item // NB, item % NB)
+                    t_f32 = t_ring.tile([P, S], F32, name="t_f32")
                     nc.vector.tensor_tensor(
                         t_f32[:],
-                        k_sb[b][:].indirect(offsets[:, j0 // 16 : (j0 + PIECE) // 16]),
-                        q_sb[b][:, half * PIECE : (half + 1) * PIECE],
+                        k_sb[b][:].indirect(offsets[:, a * S // 16 : (a + 1) * S // 16]),
+                        q_sb[b][:],
                         ALU.mult,
                     )
-                    t_bf = t_ring.tile([P, PIECE], BF16, name="t_bf")
+                    t_bf = t_ring.tile([P, S], BF16, name="t_bf")
                     nc.scalar.copy(t_bf[:], t_f32[:])
-                    if b + 1 < CB:
-                        if rest < NB:
-                            project_chunk(k_sb[b + 1], wk_sb, None, b + 1, rest)
-                        else:
-                            project_chunk(q_sb[b + 1], wq_sb, bq_sb, b + 1, rest - NB)
-                    if item % 2 == 0:
-                        project_chunk(v_sb[item // 2 // NB], wv_sb, bv_sb, item // 2 // NB, item // 2 % NB)
                     if before is not None:
                         head_sums(*before)
-                    before = (t_bf, b, a, half)
+                    before = (t_bf, b, a)
                     softmax_after(item)
-                    if item == GB * KEY_ITEMS_B + 2:
-                        for step in range(AHEAD):
-                            fetch_p(step)
                 head_sums(*before)
                 softmax_after(KEY_ITEMS)
 
             with tc.tile_pool(name="o_ring", bufs=2) as o_ring:
                 out_acc = []
 
-                def add_to_out(g, blocks):
+                def add_to_out(m, g, blocks):
                     for x in blocks:
-                        for m in range(CB):
-                            nc.tensor.matmul(
-                                out_acc[m][:],
-                                wo_sb[:, x, m * P : (m + 1) * P],
-                                ctx_bf[x][:, g * BANK : (g + 1) * BANK],
-                                start=(x == 0),
-                                stop=(x == CB - 1),
-                            )
-
-                for step in range(STEPS):
-                    b, g = block_and_chunk(step)
-                    cols = slice(g * BANK, (g + 1) * BANK)
-                    last_group = b // GB == GROUPS - 1
-                    if last_group and b % GB == 0:
-                        out_acc.clear()
-                        out_acc.extend(
-                            psum.tile([P, BANK], F32, name=f"out_acc{m}", tag="bank") for m in range(CB)
+                        nc.tensor.matmul(
+                            out_acc[m][:],
+                            wo_sb[:, x, m * P : (m + 1) * P],
+                            ctx_bf[x][:, g * BANK : (g + 1) * BANK],
+                            start=(x == 0),
+                            stop=(x == CB - 1),
                         )
-                        add_to_out(g, range(GB))
 
-                    u = u_ring.tile([P, KN, BANK], F32, name="u")
+                for step in range(len(steps)):
+                    b, n0, width = steps[step]
+                    if b == CB - 1:
+                        out_acc.clear()
+                        for m in range(CB):
+                            out_acc.append(psum.tile([P, BANK], F32, name="out_acc", tag="bank"))
+                            add_to_out(m, n0 // BANK, range(CB - 1))
+
+                    u = u_ring.tile([P, KN, WIDE], F32, name="u")
                     for a in range(KN):
-                        j0 = a * S + g * BANK
+                        j0 = a * S + n0
                         nc.vector.tensor_tensor(
-                            u[:, a, :],
-                            v_sb[b][:].indirect(offsets[:, j0 // 16 : (j0 + BANK) // 16]),
-                            p_full[step][:, a, :],
+                            u[:, a, 0:width],
+                            v_sb[b][:].indirect(offsets[:, j0 // 16 : (j0 + width) // 16]),
+                            p_full[step][:, a, 0:width],
                             ALU.mult,
                         )
-                    ctx_t = psum.tile([P, BANK // P, P], F32, name="ctx_t", tag="bank")
-                    for x in range(BANK // P):
-                        for a in range(KN):
-                            nc.tensor.matmul(
-                                ctx_t[:, x, :],
-                                u[:, a, x * P : (x + 1) * P],
-                                ident[:],
-                                start=(a == 0),
-                                stop=(a == KN - 1),
-                                is_transpose=True,
-                            )
-                    ctx_t_bf = o_ring.tile([P, BANK // P, P], BF16, name="ctx_t_bf")
-                    nc.scalar.copy(ctx_t_bf[:], ctx_t[:])
-                    ctx_ps = psum.tile([P, BANK], BF16, name="ctx_ps", tag="bank")
-                    for x in range(BANK // P):
-                        nc.tensor.transpose(ctx_ps[:, x * P : (x + 1) * P], ctx_t_bf[:, x, :], ident_bf[:])
-                    nc.scalar.copy(ctx_bf[b][:, cols], ctx_ps[:])
-                    if step + AHEAD < STEPS:
+                        softmax_after(KEY_ITEMS + 1 + step * KN + a)
+                    if step + AHEAD < len(steps):
                         fetch_p(step + AHEAD)
-                    softmax_after(KEY_ITEMS + 1 + step)
 
-                    if last_group and b % GB == GB - 1:
-                        add_to_out(g, range(GB, CB))
+                    chunks = range(width // BANK)
+                    ctx_t = [psum.tile([P, BANK // P, P], F32, name="ctx_t", tag="bank") for c in chunks]
+                    for c in chunks:
+                        for x in range(BANK // P):
+                            first = c * BANK + x * P
+                            for a in range(KN):
+                                nc.tensor.matmul(
+                                    ctx_t[c][:, x, :],
+                                    u[:, a, first : first + P],
+                                    ident[:],
+                                    start=(a == 0),
+                                    stop=(a == KN - 1),
+                                    is_transpose=True,
+                                )
+                    for c in chunks:
+                        ctx_t_bf = o_ring.tile([P, BANK // P, P], BF16, name="ctx_t_bf")
+                        nc.scalar.copy(ctx_t_bf[:], ctx_t[c][:])
+                        ctx_ps = psum.tile([P, BANK], BF16, name="ctx_ps", tag="bank")
+                        for x in range(BANK // P):
+                            nc.tensor.transpose(
+                                ctx_ps[:, x * P : (x + 1) * P], ctx_t_bf[:, x, :], ident_bf[:]
+                            )
+                        nc.scalar.copy(
+                            ctx_bf[b][:, n0 + c * BANK : n0 + (c + 1) * BANK], ctx_ps[:]
+                        )
+
+                    if b == CB - 1:
                         for m in range(CB):
-                            if m < CB - 1:
-                                o = o_ring.tile([P, BANK], F32, name="o")
-                                nc.scalar.activation(
-                                    o[:], out_acc[m][:], FUNC.Identity, bias=bo_sb[:, m : m + 1]
-                                )
-                                nc.sync.dma_start(out[m * P : (m + 1) * P, cols], o[:])
-                            else:
-                                nc.scalar.activation(
-                                    out_last[:, cols], out_acc[m][:], FUNC.Identity, bias=bo_sb[:, m : m + 1]
-                                )
-                for g in range(NB):
-                    cols = slice(g * BANK, (g + 1) * BANK)
-                    nc.sync.dma_start(out[(CB - 1) * P : CB * P, cols], out_last[:, cols])
+                            add_to_out(m, n0 // BANK, [CB - 1])
+                            o = o_ring.tile([P, BANK], F32, name="o")
+                            nc.scalar.activation(
+                                o[:], out_acc[m][:], FUNC.Identity, bias=bo_sb[:, m : m + 1]
+                            )
+                            nc.sync.dma_start(out[m * P : (m + 1) * P, n0 : n0 + BANK], o[:])

@@ -187,7 +187,8 @@ def tile_attentionfusion_b_kernel(tc, h, wq, bq, wkv, bv, wo, bo, offs, out):
                 by_head = parked(b // GB).rearrange("(a r n) -> r a n", a=KN, n=S)
                 p_full[step] = p_ring.tile([P, KN, WIDE], F32, name="p_full")
                 for hd in range(HB):
-                    nc.sync.dma_start(
+                    queue = nc.sync if hd % 2 == 0 else nc.gpsimd
+                    queue.dma_start(
                         p_full[step][hd * DK : (hd + 1) * DK, :, 0:width],
                         by_head[(b % GB) * HB + hd, :, n0 : n0 + width]
                         .unsqueeze(0)
@@ -226,7 +227,10 @@ def tile_attentionfusion_b_kernel(tc, h, wq, bq, wkv, bv, wo, bo, offs, out):
                 head_sums(*before)
                 softmax_after(KEY_ITEMS)
 
-            with tc.tile_pool(name="o_ring", bufs=2) as o_ring:
+            with (
+                tc.tile_pool(name="c_ring", bufs=2) as c_ring,
+                tc.tile_pool(name="o_ring", bufs=CB) as o_ring,
+            ):
                 out_acc = []
 
                 def add_to_out(m, g, blocks):
@@ -260,31 +264,36 @@ def tile_attentionfusion_b_kernel(tc, h, wq, bq, wkv, bv, wo, bo, offs, out):
                     if step + AHEAD < len(steps):
                         fetch_p(step + AHEAD)
 
-                    chunks = range(width // BANK)
-                    ctx_t = [psum.tile([P, BANK // P, P], F32, name="ctx_t", tag="bank") for c in chunks]
-                    for c in chunks:
-                        for x in range(BANK // P):
-                            first = c * BANK + x * P
-                            for a in range(KN):
-                                nc.tensor.matmul(
-                                    ctx_t[c][:, x, :],
-                                    u[:, a, first : first + P],
-                                    ident[:],
-                                    start=(a == 0),
-                                    stop=(a == KN - 1),
-                                    is_transpose=True,
+                    if step == len(steps) - 1:
+                        pair = c_ring.tile([P, 2, BANK], F32, name="pair")
+                        nc.vector.tensor_add(pair[:], u[:, 0:2, 0:width], u[:, 2:4, 0:width])
+                        nc.vector.tensor_add(ctx_bf[b][:, n0 : n0 + width], pair[:, 0, :], pair[:, 1, :])
+                    else:
+                        chunks = range(width // BANK)
+                        ctx_t = [psum.tile([P, BANK // P, P], F32, name="ctx_t", tag="bank") for c in chunks]
+                        for c in chunks:
+                            for x in range(BANK // P):
+                                first = c * BANK + x * P
+                                for a in range(KN):
+                                    nc.tensor.matmul(
+                                        ctx_t[c][:, x, :],
+                                        u[:, a, first : first + P],
+                                        ident[:],
+                                        start=(a == 0),
+                                        stop=(a == KN - 1),
+                                        is_transpose=True,
+                                    )
+                        for c in chunks:
+                            ctx_t_bf = c_ring.tile([P, BANK // P, P], BF16, name="ctx_t_bf")
+                            nc.scalar.copy(ctx_t_bf[:], ctx_t[c][:])
+                            ctx_ps = psum.tile([P, BANK], BF16, name="ctx_ps", tag="bank")
+                            for x in range(BANK // P):
+                                nc.tensor.transpose(
+                                    ctx_ps[:, x * P : (x + 1) * P], ctx_t_bf[:, x, :], ident_bf[:]
                                 )
-                    for c in chunks:
-                        ctx_t_bf = o_ring.tile([P, BANK // P, P], BF16, name="ctx_t_bf")
-                        nc.scalar.copy(ctx_t_bf[:], ctx_t[c][:])
-                        ctx_ps = psum.tile([P, BANK], BF16, name="ctx_ps", tag="bank")
-                        for x in range(BANK // P):
-                            nc.tensor.transpose(
-                                ctx_ps[:, x * P : (x + 1) * P], ctx_t_bf[:, x, :], ident_bf[:]
+                            nc.scalar.copy(
+                                ctx_bf[b][:, n0 + c * BANK : n0 + (c + 1) * BANK], ctx_ps[:]
                             )
-                        nc.scalar.copy(
-                            ctx_bf[b][:, n0 + c * BANK : n0 + (c + 1) * BANK], ctx_ps[:]
-                        )
 
                     if b == CB - 1:
                         for m in range(CB):

@@ -187,7 +187,7 @@ def tile_attentionfusion_b_kernel(tc, h, wq, bq, wkv, bv, wo, bo, offs, out):
                 by_head = parked(b // GB).rearrange("(a r n) -> r a n", a=KN, n=S)
                 p_full[step] = p_ring.tile([P, KN, WIDE], F32, name="p_full")
                 for hd in range(HB):
-                    queue = nc.sync if hd % 2 == 0 else nc.gpsimd
+                    queue = nc.sync if hd < HB // 2 else nc.gpsimd
                     queue.dma_start(
                         p_full[step][hd * DK : (hd + 1) * DK, :, 0:width],
                         by_head[(b % GB) * HB + hd, :, n0 : n0 + width]

@@ -25,7 +25,7 @@ GH = GB * HB
 GROUPS = CB // GB
 KEY_ITEMS = CB * KN
 WIDE = 1024
-AHEAD = 3
+AHEAD = 4
 SOFTMAX_LAG = (0, 2, 3)
 
 FLOPS = 2 * S * C * (4 * C) + 4 * C * N
@@ -36,7 +36,7 @@ def tile_attentionfusion_b_kernel(tc, h, wq, bq, wkv, bv, wo, bo, offs, out):
     with (
         tc.tile_pool(name="held", bufs=1) as held,
         tc.tile_pool(name="soft", bufs=1) as soft,
-        tc.tile_pool(name="kq_ring", bufs=2) as kq_ring,
+        tc.tile_pool(name="p_ring", bufs=AHEAD) as p_ring,
         tc.psum_pool(name="psum", bufs=8) as psum,
     ):
         offsets = held.tile([P, N // 16], U16, name="offsets")
@@ -88,23 +88,6 @@ def tile_attentionfusion_b_kernel(tc, h, wq, bq, wkv, bv, wo, bo, offs, out):
             rows = KN * GH
             first = C - (group + 1) * rows
             return out[first : first + rows, :].rearrange("x n -> (x n)")
-
-        with tc.tile_pool(name="stage", bufs=NB) as stage:
-            h_f32 = [stage.tile([P, CB, BANK], F32, name="h_f32") for n in range(NB)]
-            for n in range(NB):
-                nc.sync.dma_start(
-                    h_f32[n][:], h[:, n * BANK : (n + 1) * BANK].rearrange("(i p) n -> p i n", p=P)
-                )
-            nc.sync.dma_start(wv_sb[:], wkv[:, C : 2 * C].rearrange("(i p) r -> p i r", p=P))
-            nc.sync.dma_start(bv_sb[:], bv.rearrange("(b p) o -> p (b o)", p=P))
-            nc.sync.dma_start(wo_sb[:], wo.rearrange("(i p) m -> p i m", p=P))
-            nc.sync.dma_start(bo_sb[:], bo.rearrange("(b p) o -> p (b o)", p=P))
-            k_sb[0] = kq_ring.tile([P, S], F32, name="k_sb")
-            q_sb[0] = kq_ring.tile([P, S], F32, name="q_sb")
-            for n in range(NB):
-                nc.vector.tensor_copy(h_bf[n][:], h_f32[n][:])
-                project_chunk(k_sb[0], wk_sb, None, 0, n)
-                project_chunk(q_sb[0], wq_sb, bq_sb, 0, n)
 
         scores = []
         soft_tiles = []
@@ -176,130 +159,146 @@ def tile_attentionfusion_b_kernel(tc, h, wq, bq, wkv, bv, wo, bo, offs, out):
             steps.extend((b, n0, WIDE) for b in range(CB - 1))
             steps.extend((CB - 1, n0 + x, BANK) for x in range(0, WIDE, BANK))
 
-        with (
-            tc.tile_pool(name="p_ring", bufs=AHEAD) as p_ring,
-            tc.tile_pool(name="u_ring", bufs=2) as u_ring,
-        ):
-            p_full = {}
+        p_full = {}
 
-            def fetch_p(step):
-                b, n0, width = steps[step]
-                by_head = parked(b // GB).rearrange("(a r n) -> r a n", a=KN, n=S)
-                p_full[step] = p_ring.tile([P, KN, WIDE], F32, name="p_full")
-                for hd in range(HB):
-                    queue = nc.sync if hd < HB // 2 else nc.gpsimd
-                    queue.dma_start(
-                        p_full[step][hd * DK : (hd + 1) * DK, :, 0:width],
-                        by_head[(b % GB) * HB + hd, :, n0 : n0 + width]
-                        .unsqueeze(0)
-                        .to_broadcast([DK, KN, width]),
+        def fetch_p(step):
+            b, n0, width = steps[step]
+            by_head = parked(b // GB).rearrange("(a r n) -> r a n", a=KN, n=S)
+            p_full[step] = p_ring.tile([P, KN, WIDE], F32, name="p_full")
+            for hd in range(HB):
+                queue = nc.sync if hd < HB // 2 else nc.gpsimd
+                queue.dma_start(
+                    p_full[step][hd * DK : (hd + 1) * DK, :, 0:width],
+                    by_head[(b % GB) * HB + hd, :, n0 : n0 + width]
+                    .unsqueeze(0)
+                    .to_broadcast([DK, KN, width]),
+                )
+
+        with (
+            tc.tile_pool(name="kq_ring", bufs=2) as kq_ring,
+            tc.tile_pool(name="t_ring", bufs=2) as t_ring,
+        ):
+            h_f32 = [p_ring.tile([P, CB, BANK], F32, name="h_f32", tag="p_full") for n in range(NB)]
+            for n in range(NB):
+                nc.sync.dma_start(
+                    h_f32[n][:], h[:, n * BANK : (n + 1) * BANK].rearrange("(i p) n -> p i n", p=P)
+                )
+            nc.sync.dma_start(wv_sb[:], wkv[:, C : 2 * C].rearrange("(i p) r -> p i r", p=P))
+            nc.sync.dma_start(bv_sb[:], bv.rearrange("(b p) o -> p (b o)", p=P))
+            nc.sync.dma_start(wo_sb[:], wo.rearrange("(i p) m -> p i m", p=P))
+            nc.sync.dma_start(bo_sb[:], bo.rearrange("(b p) o -> p (b o)", p=P))
+            k_sb[0] = kq_ring.tile([P, S], F32, name="k_sb")
+            q_sb[0] = kq_ring.tile([P, S], F32, name="q_sb")
+            for n in range(NB):
+                nc.vector.tensor_copy(h_bf[n][:], h_f32[n][:])
+                project_chunk(k_sb[0], wk_sb, None, 0, n)
+                project_chunk(q_sb[0], wq_sb, bq_sb, 0, n)
+
+            before = None
+            for item in range(KEY_ITEMS):
+                b, a = divmod(item, KN)
+                if item % (GB * KN) == 0:
+                    scores.append(psum.tile([P, KN, P], F32, name="score", tag="bank"))
+                if b + 1 < CB:
+                    if a == 0:
+                        k_sb[b + 1] = kq_ring.tile([P, S], F32, name="k_sb")
+                        q_sb[b + 1] = kq_ring.tile([P, S], F32, name="q_sb")
+                    for n in (2 * a % NB, 2 * a % NB + 1):
+                        if a < KN // 2:
+                            project_chunk(k_sb[b + 1], wk_sb, None, b + 1, n)
+                        else:
+                            project_chunk(q_sb[b + 1], wq_sb, bq_sb, b + 1, n)
+                project_chunk(v_sb[item // NB], wv_sb, bv_sb, item // NB, item % NB)
+                t_f32 = t_ring.tile([P, S], F32, name="t_f32")
+                nc.vector.tensor_tensor(
+                    t_f32[:],
+                    k_sb[b][:].indirect(offsets[:, a * S // 16 : (a + 1) * S // 16]),
+                    q_sb[b][:],
+                    ALU.mult,
+                )
+                t_bf = t_ring.tile([P, S], BF16, name="t_bf")
+                nc.scalar.copy(t_bf[:], t_f32[:])
+                if before is not None:
+                    head_sums(*before)
+                before = (t_bf, b, a)
+                softmax_after(item)
+            head_sums(*before)
+            softmax_after(KEY_ITEMS)
+
+        with (
+            tc.tile_pool(name="u_ring", bufs=3) as u_ring,
+            tc.tile_pool(name="c_ring", bufs=2) as c_ring,
+            tc.tile_pool(name="o_ring", bufs=CB) as o_ring,
+        ):
+            out_acc = []
+
+            def add_to_out(m, g, blocks):
+                for x in blocks:
+                    nc.tensor.matmul(
+                        out_acc[m][:],
+                        wo_sb[:, x, m * P : (m + 1) * P],
+                        ctx_bf[x][:, g * BANK : (g + 1) * BANK],
+                        start=(x == 0),
+                        stop=(x == CB - 1),
                     )
 
-            with tc.tile_pool(name="t_ring", bufs=2) as t_ring:
-                before = None
-                for item in range(KEY_ITEMS):
-                    b, a = divmod(item, KN)
-                    if item % (GB * KN) == 0:
-                        scores.append(psum.tile([P, KN, P], F32, name="score", tag="bank"))
-                    if b + 1 < CB:
-                        if a == 0:
-                            k_sb[b + 1] = kq_ring.tile([P, S], F32, name="k_sb")
-                            q_sb[b + 1] = kq_ring.tile([P, S], F32, name="q_sb")
-                        for n in (2 * a % NB, 2 * a % NB + 1):
-                            if a < KN // 2:
-                                project_chunk(k_sb[b + 1], wk_sb, None, b + 1, n)
-                            else:
-                                project_chunk(q_sb[b + 1], wq_sb, bq_sb, b + 1, n)
-                    project_chunk(v_sb[item // NB], wv_sb, bv_sb, item // NB, item % NB)
-                    t_f32 = t_ring.tile([P, S], F32, name="t_f32")
+            for step in range(len(steps)):
+                b, n0, width = steps[step]
+                if b == CB - 1:
+                    out_acc.clear()
+                    for m in range(CB):
+                        out_acc.append(psum.tile([P, BANK], F32, name="out_acc", tag="bank"))
+                        add_to_out(m, n0 // BANK, range(CB - 1))
+
+                u = u_ring.tile([P, KN, WIDE], F32, name="u")
+                for a in range(KN):
+                    j0 = a * S + n0
                     nc.vector.tensor_tensor(
-                        t_f32[:],
-                        k_sb[b][:].indirect(offsets[:, a * S // 16 : (a + 1) * S // 16]),
-                        q_sb[b][:],
+                        u[:, a, 0:width],
+                        v_sb[b][:].indirect(offsets[:, j0 // 16 : (j0 + width) // 16]),
+                        p_full[step][:, a, 0:width],
                         ALU.mult,
                     )
-                    t_bf = t_ring.tile([P, S], BF16, name="t_bf")
-                    nc.scalar.copy(t_bf[:], t_f32[:])
-                    if before is not None:
-                        head_sums(*before)
-                    before = (t_bf, b, a)
-                    softmax_after(item)
-                head_sums(*before)
-                softmax_after(KEY_ITEMS)
+                    softmax_after(KEY_ITEMS + 1 + step * KN + a)
+                if step + AHEAD < len(steps):
+                    fetch_p(step + AHEAD)
 
-            with (
-                tc.tile_pool(name="c_ring", bufs=2) as c_ring,
-                tc.tile_pool(name="o_ring", bufs=CB) as o_ring,
-            ):
-                out_acc = []
-
-                def add_to_out(m, g, blocks):
-                    for x in blocks:
-                        nc.tensor.matmul(
-                            out_acc[m][:],
-                            wo_sb[:, x, m * P : (m + 1) * P],
-                            ctx_bf[x][:, g * BANK : (g + 1) * BANK],
-                            start=(x == 0),
-                            stop=(x == CB - 1),
-                        )
-
-                for step in range(len(steps)):
-                    b, n0, width = steps[step]
-                    if b == CB - 1:
-                        out_acc.clear()
-                        for m in range(CB):
-                            out_acc.append(psum.tile([P, BANK], F32, name="out_acc", tag="bank"))
-                            add_to_out(m, n0 // BANK, range(CB - 1))
-
-                    u = u_ring.tile([P, KN, WIDE], F32, name="u")
-                    for a in range(KN):
-                        j0 = a * S + n0
-                        nc.vector.tensor_tensor(
-                            u[:, a, 0:width],
-                            v_sb[b][:].indirect(offsets[:, j0 // 16 : (j0 + width) // 16]),
-                            p_full[step][:, a, 0:width],
-                            ALU.mult,
-                        )
-                        softmax_after(KEY_ITEMS + 1 + step * KN + a)
-                    if step + AHEAD < len(steps):
-                        fetch_p(step + AHEAD)
-
-                    if step == len(steps) - 1:
-                        pair = c_ring.tile([P, 2, BANK], F32, name="pair")
-                        nc.vector.tensor_add(pair[:], u[:, 0:2, 0:width], u[:, 2:4, 0:width])
-                        nc.vector.tensor_add(ctx_bf[b][:, n0 : n0 + width], pair[:, 0, :], pair[:, 1, :])
-                    else:
-                        chunks = range(width // BANK)
-                        ctx_t = [psum.tile([P, BANK // P, P], F32, name="ctx_t", tag="bank") for c in chunks]
-                        for c in chunks:
-                            for x in range(BANK // P):
-                                first = c * BANK + x * P
-                                for a in range(KN):
-                                    nc.tensor.matmul(
-                                        ctx_t[c][:, x, :],
-                                        u[:, a, first : first + P],
-                                        ident[:],
-                                        start=(a == 0),
-                                        stop=(a == KN - 1),
-                                        is_transpose=True,
-                                    )
-                        for c in chunks:
-                            ctx_t_bf = c_ring.tile([P, BANK // P, P], BF16, name="ctx_t_bf")
-                            nc.scalar.copy(ctx_t_bf[:], ctx_t[c][:])
-                            ctx_ps = psum.tile([P, BANK], BF16, name="ctx_ps", tag="bank")
-                            for x in range(BANK // P):
-                                nc.tensor.transpose(
-                                    ctx_ps[:, x * P : (x + 1) * P], ctx_t_bf[:, x, :], ident_bf[:]
+                if step == len(steps) - 1:
+                    pair = c_ring.tile([P, 2, BANK], F32, name="pair")
+                    nc.vector.tensor_add(pair[:], u[:, 0:2, 0:width], u[:, 2:4, 0:width])
+                    nc.vector.tensor_add(ctx_bf[b][:, n0 : n0 + width], pair[:, 0, :], pair[:, 1, :])
+                else:
+                    chunks = range(width // BANK)
+                    ctx_t = [psum.tile([P, BANK // P, P], F32, name="ctx_t", tag="bank") for c in chunks]
+                    for c in chunks:
+                        for x in range(BANK // P):
+                            first = c * BANK + x * P
+                            for a in range(KN):
+                                nc.tensor.matmul(
+                                    ctx_t[c][:, x, :],
+                                    u[:, a, first : first + P],
+                                    ident[:],
+                                    start=(a == 0),
+                                    stop=(a == KN - 1),
+                                    is_transpose=True,
                                 )
-                            nc.scalar.copy(
-                                ctx_bf[b][:, n0 + c * BANK : n0 + (c + 1) * BANK], ctx_ps[:]
+                    for c in chunks:
+                        ctx_t_bf = c_ring.tile([P, BANK // P, P], BF16, name="ctx_t_bf")
+                        nc.scalar.copy(ctx_t_bf[:], ctx_t[c][:])
+                        ctx_ps = psum.tile([P, BANK], BF16, name="ctx_ps", tag="bank")
+                        for x in range(BANK // P):
+                            nc.tensor.transpose(
+                                ctx_ps[:, x * P : (x + 1) * P], ctx_t_bf[:, x, :], ident_bf[:]
                             )
+                        nc.scalar.copy(
+                            ctx_bf[b][:, n0 + c * BANK : n0 + (c + 1) * BANK], ctx_ps[:]
+                        )
 
-                    if b == CB - 1:
-                        for m in range(CB):
-                            add_to_out(m, n0 // BANK, [CB - 1])
-                            o = o_ring.tile([P, BANK], F32, name="o")
-                            nc.scalar.activation(
-                                o[:], out_acc[m][:], FUNC.Identity, bias=bo_sb[:, m : m + 1]
-                            )
-                            nc.sync.dma_start(out[m * P : (m + 1) * P, n0 : n0 + BANK], o[:])
+                if b == CB - 1:
+                    for m in range(CB):
+                        add_to_out(m, n0 // BANK, [CB - 1])
+                        o = o_ring.tile([P, BANK], F32, name="o")
+                        nc.scalar.activation(
+                            o[:], out_acc[m][:], FUNC.Identity, bias=bo_sb[:, m : m + 1]
+                        )
+                        nc.sync.dma_start(out[m * P : (m + 1) * P, n0 : n0 + BANK], o[:])

@@ -270,16 +270,17 @@ def tile_attentionfusion_b_kernel(tc, h, wq, bq, wkv, bv, wo, bo, offs, out):
                 else:
                     chunks = range(width // BANK)
                     ctx_t = [psum.tile([P, BANK // P, P], F32, name="ctx_t", tag="bank") for c in chunks]
-                    for c in chunks:
-                        for x in range(BANK // P):
-                            first = c * BANK + x * P
-                            for a in range(KN):
+                    squares = BANK // P
+                    for a in range(KN):
+                        for c in chunks:
+                            for x in range(squares):
+                                first = c * BANK + x * P
                                 nc.tensor.matmul(
                                     ctx_t[c][:, x, :],
                                     u[:, a, first : first + P],
                                     ident[:],
-                                    start=(a == 0),
-                                    stop=(a == KN - 1),
+                                    start=(a == 0 and x == 0),
+                                    stop=(a == KN - 1 and x == squares - 1),
                                     is_transpose=True,
                                 )
                     for c in chunks:

@@ -154,9 +154,9 @@ def tile_attentionfusion_b_kernel(tc, h, wq, bq, wkv, bv, wo, bo, offs, out):
                     stop=True,
                 )
 
-        steps = []
+        steps = [(b, n0, WIDE) for n0 in range(0, S, WIDE) for b in range(GB)]
         for n0 in range(0, S, WIDE):
-            steps.extend((b, n0, WIDE) for b in range(CB - 1))
+            steps.extend((b, n0, WIDE) for b in range(GB, CB - 1))
             steps.extend((CB - 1, n0 + x, BANK) for x in range(0, WIDE, BANK))
 
         p_full = {}

@@ -26,7 +26,7 @@ GROUPS = CB // GB
 KEY_ITEMS = CB * KN
 WIDE = 1024
 AHEAD = 4
-SOFTMAX_LAG = (0, 2, 3)
+SOFTMAX_LAG = ((0, 1, 2), (0, 2, 3))
 
 FLOPS = 2 * S * C * (4 * C) + 4 * C * N
 
@@ -40,14 +40,15 @@ def tile_attentionfusion_b_kernel(tc, h, wq, bq, wkv, bv, wo, bo, offs, out):
         tc.psum_pool(name="psum", bufs=8) as psum,
     ):
         offsets = held.tile([P, N // 16], U16, name="offsets")
-        nc.sync.dma_start(offsets[:], offs)
 
+        wk_dram = wkv[:, 0:C].rearrange("(i p) r -> p i r", p=P)
+        wq_dram = wq.rearrange("(i p) c -> p i c", p=P)
+        wk_sb = held.tile([P, CB, C], BF16, name="wk_sb")
+        nc.scalar.dma_start(wk_sb[:, :, 0:P], wk_dram[:, :, 0:P])
+        wq_sb = held.tile([P, CB, C], BF16, name="wq_sb")
+        nc.scalar.dma_start(wq_sb[:, :, 0:P], wq_dram[:, :, 0:P])
         bq_sb = held.tile([P, CB], F32, name="bq_sb")
         nc.scalar.dma_start(bq_sb[:], bq.rearrange("(b p) o -> p (b o)", p=P))
-        wk_sb = held.tile([P, CB, C], BF16, name="wk_sb")
-        nc.scalar.dma_start(wk_sb[:], wkv[:, 0:C].rearrange("(i p) r -> p i r", p=P))
-        wq_sb = held.tile([P, CB, C], BF16, name="wq_sb")
-        nc.scalar.dma_start(wq_sb[:], wq.rearrange("(i p) c -> p i c", p=P))
         wv_sb = held.tile([P, CB, C], BF16, name="wv_sb")
         bv_sb = held.tile([P, CB], F32, name="bv_sb")
         wo_sb = held.tile([P, CB, C], BF16, name="wo_sb")
@@ -136,12 +137,11 @@ def tile_attentionfusion_b_kernel(tc, h, wq, bq, wkv, bv, wo, bo, offs, out):
         def softmax_after(item):
             for group in range(GROUPS):
                 lag = item - (group + 1) * GB * KN
-                if lag in SOFTMAX_LAG:
-                    softmax_stage(group, SOFTMAX_LAG.index(lag))
-                    if lag == SOFTMAX_LAG[-1]:
-                        for step in range(AHEAD):
-                            if steps[step][0] // GB == group:
-                                fetch_p(step)
+                if lag in SOFTMAX_LAG[group]:
+                    softmax_stage(group, SOFTMAX_LAG[group].index(lag))
+                    if lag == SOFTMAX_LAG[group][-1]:
+                        parked_groups.append(group)
+                        fetch_p()
 
         def head_sums(t_bf, b, a):
             by_head = scores[b // GB][:].rearrange("p a (r k) -> p a r k", k=PT)
@@ -159,20 +159,27 @@ def tile_attentionfusion_b_kernel(tc, h, wq, bq, wkv, bv, wo, bo, offs, out):
             steps.extend((b, n0, WIDE) for b in range(GB, CB - 1))
             steps.extend((CB - 1, n0 + x, BANK) for x in range(0, WIDE, BANK))
 
-        p_full = {}
+        p_full = []
+        parked_groups = []
+        spent = []
 
-        def fetch_p(step):
-            b, n0, width = steps[step]
-            by_head = parked(b // GB).rearrange("(a r n) -> r a n", a=KN, n=S)
-            p_full[step] = p_ring.tile([P, KN, WIDE], F32, name="p_full")
-            for hd in range(HB):
-                queue = nc.sync if hd < HB // 2 else nc.gpsimd
-                queue.dma_start(
-                    p_full[step][hd * DK : (hd + 1) * DK, :, 0:width],
-                    by_head[(b % GB) * HB + hd, :, n0 : n0 + width]
-                    .unsqueeze(0)
-                    .to_broadcast([DK, KN, width]),
-                )
+        def fetch_p():
+            while (
+                len(p_full) < min(len(spent) + AHEAD, len(steps))
+                and steps[len(p_full)][0] // GB in parked_groups
+            ):
+                b, n0, width = steps[len(p_full)]
+                by_head = parked(b // GB).rearrange("(a r n) -> r a n", a=KN, n=S)
+                p_tile = p_ring.tile([P, KN, WIDE], F32, name="p_full")
+                for hd in range(HB):
+                    queue = nc.sync if hd < HB // 2 else nc.gpsimd
+                    queue.dma_start(
+                        p_tile[hd * DK : (hd + 1) * DK, :, 0:width],
+                        by_head[(b % GB) * HB + hd, :, n0 : n0 + width]
+                        .unsqueeze(0)
+                        .to_broadcast([DK, KN, width]),
+                    )
+                p_full.append(p_tile)
 
         with (
             tc.tile_pool(name="kq_ring", bufs=2) as kq_ring,
@@ -183,8 +190,11 @@ def tile_attentionfusion_b_kernel(tc, h, wq, bq, wkv, bv, wo, bo, offs, out):
                 nc.sync.dma_start(
                     h_f32[n][:], h[:, n * BANK : (n + 1) * BANK].rearrange("(i p) n -> p i n", p=P)
                 )
+            nc.sync.dma_start(offsets[:], offs)
+            nc.sync.dma_start(wk_sb[:, :, P:C], wk_dram[:, :, P:C])
             nc.sync.dma_start(wv_sb[:], wkv[:, C : 2 * C].rearrange("(i p) r -> p i r", p=P))
             nc.sync.dma_start(bv_sb[:], bv.rearrange("(b p) o -> p (b o)", p=P))
+            nc.sync.dma_start(wq_sb[:, :, P:C], wq_dram[:, :, P:C])
             nc.sync.dma_start(wo_sb[:], wo.rearrange("(i p) m -> p i m", p=P))
             nc.sync.dma_start(bo_sb[:], bo.rearrange("(b p) o -> p (b o)", p=P))
             k_sb[0] = kq_ring.tile([P, S], F32, name="k_sb")
@@ -192,13 +202,13 @@ def tile_attentionfusion_b_kernel(tc, h, wq, bq, wkv, bv, wo, bo, offs, out):
             for n in range(NB):
                 nc.vector.tensor_copy(h_bf[n][:], h_f32[n][:])
                 project_chunk(k_sb[0], wk_sb, None, 0, n)
+                if n < NB // 2:
+                    project_chunk(q_sb[0], wq_sb, bq_sb, 0, n)
+            for n in range(NB // 2, NB):
                 project_chunk(q_sb[0], wq_sb, bq_sb, 0, n)
 
-            before = None
-            for item in range(KEY_ITEMS):
+            def project_beside(item):
                 b, a = divmod(item, KN)
-                if item % (GB * KN) == 0:
-                    scores.append(psum.tile([P, KN, P], F32, name="score", tag="bank"))
                 if b + 1 < CB:
                     if a == 0:
                         k_sb[b + 1] = kq_ring.tile([P, S], F32, name="k_sb")
@@ -209,18 +219,30 @@ def tile_attentionfusion_b_kernel(tc, h, wq, bq, wkv, bv, wo, bo, offs, out):
                         else:
                             project_chunk(q_sb[b + 1], wq_sb, bq_sb, b + 1, n)
                 project_chunk(v_sb[item // NB], wv_sb, bv_sb, item // NB, item % NB)
+
+            before = None
+            project_beside(0)
+            for item in range(KEY_ITEMS):
+                b, a = divmod(item, KN)
+                if item % (GB * KN) == 0:
+                    scores.append(psum.tile([P, KN, P], F32, name="score", tag="bank"))
                 t_f32 = t_ring.tile([P, S], F32, name="t_f32")
-                nc.vector.tensor_tensor(
-                    t_f32[:],
-                    k_sb[b][:].indirect(offsets[:, a * S // 16 : (a + 1) * S // 16]),
-                    q_sb[b][:],
-                    ALU.mult,
-                )
+                width = S // 2 if item == 0 else S
+                for n0 in range(0, S, width):
+                    j0 = a * S + n0
+                    nc.vector.tensor_tensor(
+                        t_f32[:, n0 : n0 + width],
+                        k_sb[b][:].indirect(offsets[:, j0 // 16 : (j0 + width) // 16]),
+                        q_sb[b][:, n0 : n0 + width],
+                        ALU.mult,
+                    )
                 t_bf = t_ring.tile([P, S], BF16, name="t_bf")
                 nc.scalar.copy(t_bf[:], t_f32[:])
                 if before is not None:
                     head_sums(*before)
                 before = (t_bf, b, a)
+                if item + 1 < KEY_ITEMS:
+                    project_beside(item + 1)
                 softmax_after(item)
             head_sums(*before)
             softmax_after(KEY_ITEMS)
@@ -260,8 +282,8 @@ def tile_attentionfusion_b_kernel(tc, h, wq, bq, wkv, bv, wo, bo, offs, out):
                         ALU.mult,
                     )
                     softmax_after(KEY_ITEMS + 1 + step * KN + a)
-                if step + AHEAD < len(steps):
-                    fetch_p(step + AHEAD)
+                spent.append(step)
+                fetch_p()
 
                 if step == len(steps) - 1:
                     pair = c_ring.tile([P, 2, BANK], F32, name="pair")

@@ -7,6 +7,7 @@ F32 = mybir.dt.float32
 BF16 = mybir.dt.bfloat16
 U16 = mybir.dt.uint16
 ALU = mybir.AluOpType
+AXIS = mybir.AxisListType
 FUNC = mybir.ActivationFunctionType
 
 P = 128
@@ -98,7 +99,6 @@ def tile_attentionfusion_b_kernel(tc, h, wq, bq, wkv, bv, wo, bo, offs, out):
                 soft_tiles.append(
                     {
                         "sc": soft.tile([P, KN, P], F32, name="sc"),
-                        "max2": soft.tile([P, 2, P], F32, name="max2"),
                         "max1": soft.tile([P, P], F32, name="max1"),
                         "e": soft.tile([P, KN, P], F32, name="e"),
                         "sum2": soft.tile([P, 2, P], F32, name="sum2"),
@@ -110,15 +110,14 @@ def tile_attentionfusion_b_kernel(tc, h, wq, bq, wkv, bv, wo, bo, offs, out):
                 )
             t = soft_tiles[group]
             over_slots = [P, KN, P]
-            if stage == 0:
-                nc.scalar.mul(t["sc"][:], scores[group][:], 1.0 / math.sqrt(DK))
             if stage == 1:
-                nc.vector.tensor_max(t["max2"][:], t["sc"][:, 0:2, :], t["sc"][:, 2:4, :])
-                nc.vector.tensor_max(t["max1"][:], t["max2"][:, 0, :], t["max2"][:, 1, :])
-                nc.vector.tensor_sub(
-                    t["sc"][:], t["sc"][:], t["max1"][:].unsqueeze(1).to_broadcast(over_slots)
+                nc.vector.tensor_reduce(
+                    t["max1"][:], scores[group][:].rearrange("p a c -> p c a"), AXIS.X, ALU.max
                 )
-                nc.scalar.activation(t["e"][:], t["sc"][:], FUNC.Exp)
+                nc.vector.tensor_sub(
+                    t["sc"][:], scores[group][:], t["max1"][:].unsqueeze(1).to_broadcast(over_slots)
+                )
+                nc.scalar.activation(t["e"][:], t["sc"][:], FUNC.Exp, scale=1.0 / math.sqrt(DK))
             if stage == 2:
                 nc.vector.tensor_add(t["sum2"][:], t["e"][:, 0:2, :], t["e"][:, 2:4, :])
                 nc.vector.tensor_add(t["sum1"][:], t["sum2"][:, 0, :], t["sum2"][:, 1, :])
@@ -321,7 +320,10 @@ def tile_attentionfusion_b_kernel(tc, h, wq, bq, wkv, bv, wo, bo, offs, out):
                     for m in range(CB):
                         add_to_out(m, n0 // BANK, [CB - 1])
                         o = o_ring.tile([P, BANK], F32, name="o")
-                        nc.scalar.activation(
-                            o[:], out_acc[m][:], FUNC.Identity, bias=bo_sb[:, m : m + 1]
-                        )
+                        if step == len(steps) - 1 and m % 2 == 1:
+                            nc.vector.tensor_scalar_add(o[:], out_acc[m][:], bo_sb[:, m : m + 1])
+                        else:
+                            nc.scalar.activation(
+                                o[:], out_acc[m][:], FUNC.Identity, bias=bo_sb[:, m : m + 1]
+                            )
                         nc.sync.dma_start(out[m * P : (m + 1) * P, n0 : n0 + BANK], o[:])

@@ -22,12 +22,12 @@ BANK = 512
 NB = S // BANK
 PT = S // P
 GB = 2
-GH = GB * HB
-GROUPS = CB // GB
+PAIRS = KN * KN
+BANK_TILES = BANK // (PAIRS * HB)
+TILE_SETS = PT // BANK_TILES
 KEY_ITEMS = CB * KN
 WIDE = 1024
 AHEAD = 4
-SOFTMAX_LAG = ((0, 1, 2), (0, 2, 3))
 
 FLOPS = 2 * S * C * (4 * C) + 4 * C * N
 
@@ -36,7 +36,8 @@ def tile_attentionfusion_b_kernel(tc, h, wq, bq, wkv, bv, wo, bo, offs, out):
     nc = tc.nc
     with (
         tc.tile_pool(name="held", bufs=1) as held,
-        tc.tile_pool(name="soft", bufs=1) as soft,
+        tc.tile_pool(name="soft", bufs=2) as soft,
+        tc.tile_pool(name="park", bufs=1) as park,
         tc.tile_pool(name="p_ring", bufs=AHEAD) as p_ring,
         tc.psum_pool(name="psum", bufs=8) as psum,
     ):
@@ -59,6 +60,19 @@ def tile_attentionfusion_b_kernel(tc, h, wq, bq, wkv, bv, wo, bo, offs, out):
         nc.vector.memset(head_sel[:], 0.0)
         for hd in range(HB):
             nc.vector.memset(head_sel[hd * DK : (hd + 1) * DK, hd : hd + 1], 1.0)
+        coef = held.tile([P, KN, KN, KN], BF16, name="coef")
+        nc.vector.memset(coef[:], 0.0)
+        for a in range(KN):
+            nc.vector.memset(coef[:, a, a, :], 1.0)
+            nc.vector.memset(coef[:, a, :, a], -1.0)
+            nc.vector.memset(coef[:, a, a, a : a + 1], 0.0)
+        pair_sel = held.tile([P, KN, PAIRS * HB], BF16, name="pair_sel")
+        nc.vector.tensor_tensor(
+            pair_sel[:].rearrange("p a (z r) -> p (a z) r", r=HB),
+            coef[:].rearrange("p a x y -> p (a x y)").unsqueeze(2).to_broadcast([P, KN * PAIRS, HB]),
+            head_sel[:].unsqueeze(1).to_broadcast([P, KN * PAIRS, HB]),
+            ALU.mult,
+        )
         ident = held.tile([P, P], F32, name="ident")
         make_identity(nc, ident[:])
         ident_bf = held.tile([P, P], BF16, name="ident_bf")
@@ -86,72 +100,73 @@ def tile_attentionfusion_b_kernel(tc, h, wq, bq, wkv, bv, wo, bo, offs, out):
             else:
                 nc.scalar.activation(dst[:, cols], acc[:], FUNC.Identity, bias=bias[:, b : b + 1])
 
-        def parked(group):
-            rows = KN * GH
-            first = C - (group + 1) * rows
-            return out[first : first + rows, :].rearrange("x n -> (x n)")
+        def parked(first_block, blocks):
+            rows = KN * HB
+            first = C - CB * rows + first_block * rows
+            return out[first : first + blocks * rows, :].rearrange("x n -> (x n)")
 
-        scores = []
-        soft_tiles = []
+        diffs = {}
+        exps = {}
+        sums = {}
 
-        def softmax_stage(group, stage):
-            if stage == 0:
-                soft_tiles.append(
-                    {
-                        "sc": soft.tile([P, KN, P], F32, name="sc"),
-                        "max1": soft.tile([P, P], F32, name="max1"),
-                        "e": soft.tile([P, KN, P], F32, name="e"),
-                        "sum2": soft.tile([P, 2, P], F32, name="sum2"),
-                        "sum1": soft.tile([P, P], F32, name="sum1"),
-                        "inv": soft.tile([P, P], F32, name="inv"),
-                        "p": soft.tile([P, KN, P], F32, name="p"),
-                        "p_rows": soft.tile([P, KN, P], F32, name="p_rows"),
-                    }
-                )
-            t = soft_tiles[group]
-            over_slots = [P, KN, P]
-            if stage == 1:
-                nc.vector.tensor_reduce(
-                    t["max1"][:], scores[group][:].rearrange("p a c -> p c a"), AXIS.X, ALU.max
-                )
-                nc.vector.tensor_sub(
-                    t["sc"][:], scores[group][:], t["max1"][:].unsqueeze(1).to_broadcast(over_slots)
-                )
-                nc.scalar.activation(t["e"][:], t["sc"][:], FUNC.Exp, scale=1.0 / math.sqrt(DK))
-            if stage == 2:
-                nc.vector.tensor_add(t["sum2"][:], t["e"][:, 0:2, :], t["e"][:, 2:4, :])
-                nc.vector.tensor_add(t["sum1"][:], t["sum2"][:, 0, :], t["sum2"][:, 1, :])
-                nc.vector.reciprocal(t["inv"][:], t["sum1"][:])
-                nc.vector.tensor_mul(
-                    t["p"][:], t["e"][:], t["inv"][:].unsqueeze(1).to_broadcast(over_slots)
-                )
-                flipped = psum.tile([P, KN, P], F32, name="flipped", tag="bank")
-                for a in range(KN):
-                    nc.tensor.transpose(flipped[:, a, :], t["p"][:, a, :], ident[:])
-                nc.scalar.copy(t["p_rows"][:], flipped[:])
-                nc.sync.dma_start(
-                    parked(group).rearrange("(a r w) -> r a w", a=KN, w=P), t["p_rows"][:]
-                )
-
-        def softmax_after(item):
-            for group in range(GROUPS):
-                lag = item - (group + 1) * GB * KN
-                if lag in SOFTMAX_LAG[group]:
-                    softmax_stage(group, SOFTMAX_LAG[group].index(lag))
-                    if lag == SOFTMAX_LAG[group][-1]:
-                        parked_groups.append(group)
-                        fetch_p()
-
-        def head_sums(t_bf, b, a):
-            by_head = scores[b // GB][:].rearrange("p a (r k) -> p a r k", k=PT)
+        def pair_sums(t_bf, b, a):
+            if a == 0:
+                diffs[b] = [
+                    psum.tile([P, PAIRS * HB, BANK_TILES], F32, name="diff", tag="bank")
+                    for s in range(TILE_SETS)
+                ]
             for k in range(PT):
                 nc.tensor.matmul(
-                    by_head[:, a, (b % GB) * HB : (b % GB + 1) * HB, k],
+                    diffs[b][k % TILE_SETS][:, :, k // TILE_SETS],
                     t_bf[:, k * P : (k + 1) * P],
-                    head_sel[:],
-                    start=True,
-                    stop=True,
+                    pair_sel[:, a, :],
+                    start=(a == 0 and k // TILE_SETS == 0),
+                    stop=(a == KN - 1 and k // TILE_SETS == BANK_TILES - 1),
                 )
+
+        def softmax_exp(b):
+            exps[b] = soft.tile([P, TILE_SETS, BANK], F32, name="e")
+            for s in range(TILE_SETS):
+                nc.scalar.activation(
+                    exps[b][:, s, :],
+                    diffs[b][s][:].rearrange("p z k -> p (z k)"),
+                    FUNC.Exp,
+                    scale=1.0 / math.sqrt(DK),
+                )
+
+        def softmax_flip(b):
+            if b % GB == 0:
+                sums[b // GB] = psum.tile([P, GB, TILE_SETS, P], F32, name="z_rows", tag="bank")
+            for s in range(TILE_SETS):
+                for x in range(KN):
+                    nc.tensor.matmul(
+                        sums[b // GB][:, b % GB, s, :],
+                        exps[b][:, s, x * P : (x + 1) * P],
+                        ident[:],
+                        start=(s == 0 and x == 0),
+                        stop=(s == TILE_SETS - 1 and x == KN - 1),
+                        is_transpose=True,
+                    )
+
+        def softmax_park(group):
+            ln_z = park.tile([P, GB, TILE_SETS * P], F32, name="ln_z")
+            nc.scalar.activation(ln_z[:], sums[group][:].rearrange("p j s w -> p j (s w)"), FUNC.Ln)
+            p_rows = park.tile([P, GB, TILE_SETS * P], F32, name="p_rows")
+            nc.scalar.activation(p_rows[:], ln_z[:], FUNC.Exp, scale=-1.0)
+            nc.sync.dma_start(
+                parked(group * GB, GB).rearrange("(j r v) -> r j v", j=GB, v=TILE_SETS * P), p_rows[:]
+            )
+            parked_blocks.extend(range(group * GB, (group + 1) * GB))
+            fetch_p()
+
+        def softmax_after(item):
+            b, lag = divmod(item, KN)
+            if b >= 1 and lag == 0:
+                softmax_exp(b - 1)
+            if b >= 1 and lag == 1:
+                softmax_flip(b - 1)
+            if b >= 1 and lag == 2 and b % GB == 0:
+                softmax_park(b // GB - 1)
 
         steps = [(b, n0, WIDE) for n0 in range(0, S, WIDE) for b in range(GB)]
         for n0 in range(0, S, WIDE):
@@ -159,26 +174,30 @@ def tile_attentionfusion_b_kernel(tc, h, wq, bq, wkv, bv, wo, bo, offs, out):
             steps.extend((CB - 1, n0 + x, BANK) for x in range(0, WIDE, BANK))
 
         p_full = []
-        parked_groups = []
+        parked_blocks = []
         spent = []
 
         def fetch_p():
             while (
                 len(p_full) < min(len(spent) + AHEAD, len(steps))
-                and steps[len(p_full)][0] // GB in parked_groups
+                and steps[len(p_full)][0] in parked_blocks
             ):
                 b, n0, width = steps[len(p_full)]
-                by_head = parked(b // GB).rearrange("(a r n) -> r a n", a=KN, n=S)
+                by_head = parked(b, 1).rearrange("(a r n) -> r a n", a=KN, n=S)
                 p_tile = p_ring.tile([P, KN, WIDE], F32, name="p_full")
                 for hd in range(HB):
                     queue = nc.sync if hd < HB // 2 else nc.gpsimd
                     queue.dma_start(
                         p_tile[hd * DK : (hd + 1) * DK, :, 0:width],
-                        by_head[(b % GB) * HB + hd, :, n0 : n0 + width]
+                        by_head[hd, :, n0 : n0 + width]
                         .unsqueeze(0)
                         .to_broadcast([DK, KN, width]),
                     )
                 p_full.append(p_tile)
+
+        def project_values(first):
+            for x in (first, first + 1):
+                project_chunk(v_sb[x // NB], wv_sb, bv_sb, x // NB, x % NB)
 
         with (
             tc.tile_pool(name="kq_ring", bufs=2) as kq_ring,
@@ -217,14 +236,13 @@ def tile_attentionfusion_b_kernel(tc, h, wq, bq, wkv, bv, wo, bo, offs, out):
                             project_chunk(k_sb[b + 1], wk_sb, None, b + 1, n)
                         else:
                             project_chunk(q_sb[b + 1], wq_sb, bq_sb, b + 1, n)
-                project_chunk(v_sb[item // NB], wv_sb, bv_sb, item // NB, item % NB)
+                else:
+                    project_values(2 * a)
 
             before = None
             project_beside(0)
             for item in range(KEY_ITEMS):
                 b, a = divmod(item, KN)
-                if item % (GB * KN) == 0:
-                    scores.append(psum.tile([P, KN, P], F32, name="score", tag="bank"))
                 t_f32 = t_ring.tile([P, S], F32, name="t_f32")
                 width = S // 2 if item == 0 else S
                 for n0 in range(0, S, width):
@@ -238,13 +256,13 @@ def tile_attentionfusion_b_kernel(tc, h, wq, bq, wkv, bv, wo, bo, offs, out):
                 t_bf = t_ring.tile([P, S], BF16, name="t_bf")
                 nc.scalar.copy(t_bf[:], t_f32[:])
                 if before is not None:
-                    head_sums(*before)
+                    pair_sums(*before)
                 before = (t_bf, b, a)
                 if item + 1 < KEY_ITEMS:
                     project_beside(item + 1)
                 softmax_after(item)
-            head_sums(*before)
-            softmax_after(KEY_ITEMS)
+            pair_sums(*before)
+            softmax_exp(CB - 1)
 
         with (
             tc.tile_pool(name="u_ring", bufs=3) as u_ring,
@@ -265,6 +283,8 @@ def tile_attentionfusion_b_kernel(tc, h, wq, bq, wkv, bv, wo, bo, offs, out):
 
             for step in range(len(steps)):
                 b, n0, width = steps[step]
+                if step < GB * S // WIDE:
+                    project_values(GB * NB + 2 * step)
                 if b == CB - 1:
                     out_acc.clear()
                     for m in range(CB):
@@ -280,7 +300,6 @@ def tile_attentionfusion_b_kernel(tc, h, wq, bq, wkv, bv, wo, bo, offs, out):
                         p_full[step][:, a, 0:width],
                         ALU.mult,
                     )
-                    softmax_after(KEY_ITEMS + 1 + step * KN + a)
                 spent.append(step)
                 fetch_p()
 
@@ -304,6 +323,8 @@ def tile_attentionfusion_b_kernel(tc, h, wq, bq, wkv, bv, wo, bo, offs, out):
                                     stop=(a == KN - 1 and x == squares - 1),
                                     is_transpose=True,
                                 )
+                    if step == 0:
+                        softmax_flip(CB - 1)
                     for c in chunks:
                         ctx_t_bf = c_ring.tile([P, BANK // P, P], BF16, name="ctx_t_bf")
                         nc.scalar.copy(ctx_t_bf[:], ctx_t[c][:])
@@ -315,6 +336,8 @@ def tile_attentionfusion_b_kernel(tc, h, wq, bq, wkv, bv, wo, bo, offs, out):
                         nc.scalar.copy(
                             ctx_bf[b][:, n0 + c * BANK : n0 + (c + 1) * BANK], ctx_ps[:]
                         )
+                    if step == 0:
+                        softmax_park(CB // GB - 1)
 
                 if b == CB - 1:
                     for m in range(CB):

@@ -39,6 +39,7 @@ def tile_attentionfusion_b_kernel(tc, h, wq, bq, wkv, bv, wo, bo, offs, out):
         tc.tile_pool(name="soft", bufs=2) as soft,
         tc.tile_pool(name="park", bufs=1) as park,
         tc.tile_pool(name="p_ring", bufs=AHEAD) as p_ring,
+        tc.tile_pool(name="product_ring", bufs=3) as product_ring,
         tc.psum_pool(name="psum", bufs=8) as psum,
     ):
         offsets = held.tile([P, N // 16], U16, name="offsets")
@@ -82,7 +83,6 @@ def tile_attentionfusion_b_kernel(tc, h, wq, bq, wkv, bv, wo, bo, offs, out):
         k_sb = {}
         q_sb = {}
         v_sb = [held.tile([P, S], F32, name=f"v_sb{b}") for b in range(CB)]
-        ctx_bf = [held.tile([P, S], BF16, name=f"ctx_bf{b}") for b in range(CB)]
 
         def project_chunk(dst, w_sb, bias, b, n):
             acc = psum.tile([P, BANK], F32, name="acc", tag="bank")
@@ -195,9 +195,12 @@ def tile_attentionfusion_b_kernel(tc, h, wq, bq, wkv, bv, wo, bo, offs, out):
                     )
                 p_full.append(p_tile)
 
-        def project_values(first):
-            for x in (first, first + 1):
+        v_made = []
+
+        def project_values(count):
+            for x in range(len(v_made), len(v_made) + count):
                 project_chunk(v_sb[x // NB], wv_sb, bv_sb, x // NB, x % NB)
+                v_made.append(x)
 
         with (
             tc.tile_pool(name="kq_ring", bufs=2) as kq_ring,
@@ -236,14 +239,16 @@ def tile_attentionfusion_b_kernel(tc, h, wq, bq, wkv, bv, wo, bo, offs, out):
                             project_chunk(k_sb[b + 1], wk_sb, None, b + 1, n)
                         else:
                             project_chunk(q_sb[b + 1], wq_sb, bq_sb, b + 1, n)
+                    if item >= KEY_ITEMS - KN - (CB * NB - 3 * KN):
+                        project_values(1)
                 else:
-                    project_values(2 * a)
+                    project_values(3)
 
             before = None
             project_beside(0)
             for item in range(KEY_ITEMS):
                 b, a = divmod(item, KN)
-                t_f32 = t_ring.tile([P, S], F32, name="t_f32")
+                t_f32 = product_ring.tile([P, S], F32, name="t_f32", tag="product")
                 width = S // 2 if item == 0 else S
                 for n0 in range(0, S, width):
                     j0 = a * S + n0
@@ -265,10 +270,11 @@ def tile_attentionfusion_b_kernel(tc, h, wq, bq, wkv, bv, wo, bo, offs, out):
             softmax_exp(CB - 1)
 
         with (
-            tc.tile_pool(name="u_ring", bufs=3) as u_ring,
+            tc.tile_pool(name="ctx_pool", bufs=1) as ctx_pool,
             tc.tile_pool(name="c_ring", bufs=2) as c_ring,
             tc.tile_pool(name="o_ring", bufs=CB) as o_ring,
         ):
+            ctx_bf = [ctx_pool.tile([P, S], BF16, name=f"ctx_bf{b}") for b in range(CB)]
             out_acc = []
 
             def add_to_out(m, g, blocks):
@@ -283,15 +289,13 @@ def tile_attentionfusion_b_kernel(tc, h, wq, bq, wkv, bv, wo, bo, offs, out):
 
             for step in range(len(steps)):
                 b, n0, width = steps[step]
-                if step < GB * S // WIDE:
-                    project_values(GB * NB + 2 * step)
                 if b == CB - 1:
                     out_acc.clear()
                     for m in range(CB):
                         out_acc.append(psum.tile([P, BANK], F32, name="out_acc", tag="bank"))
                         add_to_out(m, n0 // BANK, range(CB - 1))
 
-                u = u_ring.tile([P, KN, WIDE], F32, name="u")
+                u = product_ring.tile([P, KN, WIDE], F32, name="u", tag="product")
                 for a in range(KN):
                     j0 = a * S + n0
                     nc.vector.tensor_tensor(

@@ -207,11 +207,15 @@ def tile_attentionfusion_b_kernel(tc, h, wq, bq, wkv, bv, wo, bo, offs, out):
             tc.tile_pool(name="t_ring", bufs=2) as t_ring,
         ):
             h_f32 = [p_ring.tile([P, CB, BANK], F32, name="h_f32", tag="p_full") for n in range(NB)]
-            for n in range(NB):
+            for n in range(NB - 1):
                 nc.sync.dma_start(
                     h_f32[n][:], h[:, n * BANK : (n + 1) * BANK].rearrange("(i p) n -> p i n", p=P)
                 )
             nc.sync.dma_start(offsets[:], offs)
+            for i in range(CB):
+                nc.sync.dma_start(
+                    h_f32[NB - 1][:, i, :], h[i * P : (i + 1) * P, (NB - 1) * BANK : NB * BANK]
+                )
             nc.sync.dma_start(wk_sb[:, :, P:C], wk_dram[:, :, P:C])
             nc.sync.dma_start(wv_sb[:], wkv[:, C : 2 * C].rearrange("(i p) r -> p i r", p=P))
             nc.sync.dma_start(bv_sb[:], bv.rearrange("(b p) o -> p (b o)", p=P))
@@ -221,7 +225,8 @@ def tile_attentionfusion_b_kernel(tc, h, wq, bq, wkv, bv, wo, bo, offs, out):
             k_sb[0] = kq_ring.tile([P, S], F32, name="k_sb")
             q_sb[0] = kq_ring.tile([P, S], F32, name="q_sb")
             for n in range(NB):
-                nc.vector.tensor_copy(h_bf[n][:], h_f32[n][:])
+                for i in range(CB):
+                    nc.vector.tensor_copy(h_bf[n][:, i, :], h_f32[n][:, i, :])
                 project_chunk(k_sb[0], wk_sb, None, 0, n)
                 if n < NB // 2:
                     project_chunk(q_sb[0], wq_sb, bq_sb, 0, n)

@@ -28,6 +28,7 @@ TILE_SETS = PT // BANK_TILES
 KEY_ITEMS = CB * KN
 WIDE = 1024
 AHEAD = 4
+VECTOR_SUMS = 2
 
 FLOPS = 2 * S * C * (4 * C) + 4 * C * N
 
@@ -312,7 +313,7 @@ def tile_attentionfusion_b_kernel(tc, h, wq, bq, wkv, bv, wo, bo, offs, out):
                 spent.append(step)
                 fetch_p()
 
-                if step == len(steps) - 1:
+                if step >= len(steps) - VECTOR_SUMS:
                     pair = c_ring.tile([P, 2, BANK], F32, name="pair")
                     nc.vector.tensor_add(pair[:], u[:, 0:2, 0:width], u[:, 2:4, 0:width])
                     nc.vector.tensor_add(ctx_bf[b][:, n0 : n0 + width], pair[:, 0, :], pair[:, 1, :])

@@ -28,7 +28,7 @@ TILE_SETS = PT // BANK_TILES
 KEY_ITEMS = CB * KN
 WIDE = 1024
 AHEAD = 4
-VECTOR_SUMS = 2
+VECTOR_SUMS = 3
 
 FLOPS = 2 * S * C * (4 * C) + 4 * C * N
 
@@ -172,7 +172,11 @@ def tile_attentionfusion_b_kernel(tc, h, wq, bq, wkv, bv, wo, bo, offs, out):
         steps = [(b, n0, WIDE) for n0 in range(0, S, WIDE) for b in range(GB)]
         for n0 in range(0, S, WIDE):
             steps.extend((b, n0, WIDE) for b in range(GB, CB - 1))
-            steps.extend((CB - 1, n0 + x, BANK) for x in range(0, WIDE, BANK))
+            steps.append((CB - 1, n0, BANK))
+            if n0 + WIDE < S:
+                steps.append((CB - 1, n0 + BANK, BANK))
+            else:
+                steps.extend((CB - 1, n0 + BANK + x, BANK // 2) for x in (0, BANK // 2))
 
         p_full = []
         parked_blocks = []
@@ -278,17 +282,17 @@ def tile_attentionfusion_b_kernel(tc, h, wq, bq, wkv, bv, wo, bo, offs, out):
         with (
             tc.tile_pool(name="ctx_pool", bufs=1) as ctx_pool,
             tc.tile_pool(name="c_ring", bufs=2) as c_ring,
-            tc.tile_pool(name="o_ring", bufs=CB) as o_ring,
+            tc.tile_pool(name="o_ring", bufs=2 * CB) as o_ring,
         ):
             ctx_bf = [ctx_pool.tile([P, S], BF16, name=f"ctx_bf{b}") for b in range(CB)]
             out_acc = []
 
-            def add_to_out(m, g, blocks):
+            def add_to_out(m, n0, width, blocks):
                 for x in blocks:
                     nc.tensor.matmul(
-                        out_acc[m][:],
+                        out_acc[m][:, 0:width],
                         wo_sb[:, x, m * P : (m + 1) * P],
-                        ctx_bf[x][:, g * BANK : (g + 1) * BANK],
+                        ctx_bf[x][:, n0 : n0 + width],
                         start=(x == 0),
                         stop=(x == CB - 1),
                     )
@@ -299,9 +303,10 @@ def tile_attentionfusion_b_kernel(tc, h, wq, bq, wkv, bv, wo, bo, offs, out):
                     out_acc.clear()
                     for m in range(CB):
                         out_acc.append(psum.tile([P, BANK], F32, name="out_acc", tag="bank"))
-                        add_to_out(m, n0 // BANK, range(CB - 1))
+                        add_to_out(m, n0, width, range(CB - 1))
 
                 u = product_ring.tile([P, KN, WIDE], F32, name="u", tag="product")
+                total = u[:, 0, 0:width]
                 for a in range(KN):
                     j0 = a * S + n0
                     nc.vector.tensor_tensor(
@@ -310,21 +315,26 @@ def tile_attentionfusion_b_kernel(tc, h, wq, bq, wkv, bv, wo, bo, offs, out):
                         p_full[step][:, a, 0:width],
                         ALU.mult,
                     )
+                    if step >= len(steps) - VECTOR_SUMS and a > 0:
+                        if a < KN - 1:
+                            part = c_ring.tile([P, BANK], F32, name="part")
+                            new_total = part[:, 0:width]
+                        else:
+                            new_total = ctx_bf[b][:, n0 : n0 + width]
+                        nc.vector.tensor_add(new_total, total, u[:, a, 0:width])
+                        total = new_total
                 spent.append(step)
                 fetch_p()
 
-                if step >= len(steps) - VECTOR_SUMS:
-                    pair = c_ring.tile([P, 2, BANK], F32, name="pair")
-                    nc.vector.tensor_add(pair[:], u[:, 0:2, 0:width], u[:, 2:4, 0:width])
-                    nc.vector.tensor_add(ctx_bf[b][:, n0 : n0 + width], pair[:, 0, :], pair[:, 1, :])
-                else:
-                    chunks = range(width // BANK)
+                if step < len(steps) - VECTOR_SUMS:
+                    piece = min(width, BANK)
+                    chunks = range(width // piece)
                     ctx_t = [psum.tile([P, BANK // P, P], F32, name="ctx_t", tag="bank") for c in chunks]
-                    squares = BANK // P
+                    squares = piece // P
                     for a in range(KN):
                         for c in chunks:
                             for x in range(squares):
-                                first = c * BANK + x * P
+                                first = c * piece + x * P
                                 nc.tensor.matmul(
                                     ctx_t[c][:, x, :],
                                     u[:, a, first : first + P],
@@ -337,26 +347,31 @@ def tile_attentionfusion_b_kernel(tc, h, wq, bq, wkv, bv, wo, bo, offs, out):
                         softmax_flip(CB - 1)
                     for c in chunks:
                         ctx_t_bf = c_ring.tile([P, BANK // P, P], BF16, name="ctx_t_bf")
-                        nc.scalar.copy(ctx_t_bf[:], ctx_t[c][:])
+                        nc.scalar.copy(ctx_t_bf[:, 0:squares, :], ctx_t[c][:, 0:squares, :])
                         ctx_ps = psum.tile([P, BANK], BF16, name="ctx_ps", tag="bank")
-                        for x in range(BANK // P):
+                        for x in range(squares):
                             nc.tensor.transpose(
                                 ctx_ps[:, x * P : (x + 1) * P], ctx_t_bf[:, x, :], ident_bf[:]
                             )
                         nc.scalar.copy(
-                            ctx_bf[b][:, n0 + c * BANK : n0 + (c + 1) * BANK], ctx_ps[:]
+                            ctx_bf[b][:, n0 + c * piece : n0 + (c + 1) * piece], ctx_ps[:, 0:piece]
                         )
                     if step == 0:
                         softmax_park(CB // GB - 1)
 
                 if b == CB - 1:
                     for m in range(CB):
-                        add_to_out(m, n0 // BANK, [CB - 1])
+                        add_to_out(m, n0, width, [CB - 1])
                         o = o_ring.tile([P, BANK], F32, name="o")
                         if step == len(steps) - 1 and m % 2 == 1:
-                            nc.vector.tensor_scalar_add(o[:], out_acc[m][:], bo_sb[:, m : m + 1])
+                            nc.vector.tensor_scalar_add(
+                                o[:, 0:width], out_acc[m][:, 0:width], bo_sb[:, m : m + 1]
+                            )
                         else:
                             nc.scalar.activation(
-                                o[:], out_acc[m][:], FUNC.Identity, bias=bo_sb[:, m : m + 1]
+                                o[:, 0:width],
+                                out_acc[m][:, 0:width],
+                                FUNC.Identity,
+                                bias=bo_sb[:, m : m + 1],
                             )
-                        nc.sync.dma_start(out[m * P : (m + 1) * P, n0 : n0 + BANK], o[:])
+                        nc.sync.dma_start(out[m * P : (m + 1) * P, n0 : n0 + width], o[:, 0:width])

import math

import concourse.mybir as mybir
from concourse.masks import make_identity

F32 = mybir.dt.float32
BF16 = mybir.dt.bfloat16
U16 = mybir.dt.uint16
ALU = mybir.AluOpType
AXIS = mybir.AxisListType
FUNC = mybir.ActivationFunctionType

P = 128
C = 512
CB = C // P
S = 2048
KN = 4
DK = 32
HB = P // DK
N = KN * S
BANK = 512
NB = S // BANK
PT = S // P
GB = 2
PAIRS = KN * KN
BANK_TILES = BANK // (PAIRS * HB)
TILE_SETS = PT // BANK_TILES
KEY_ITEMS = CB * KN
WIDE = 1024
AHEAD = 4
VECTOR_SUMS = 3

FLOPS = 2 * S * C * (4 * C) + 4 * C * N


def tile_attentionfusion_b_kernel(tc, h, wq, bq, wkv, bv, wo, bo, offs, out):
    nc = tc.nc
    with (
        tc.tile_pool(name="held", bufs=1) as held,
        tc.tile_pool(name="soft", bufs=2) as soft,
        tc.tile_pool(name="park", bufs=1) as park,
        tc.tile_pool(name="p_ring", bufs=AHEAD) as p_ring,
        tc.tile_pool(name="product_ring", bufs=3) as product_ring,
        tc.psum_pool(name="psum", bufs=8) as psum,
    ):
        offsets = held.tile([P, N // 16], U16, name="offsets")

        wk_dram = wkv[:, 0:C].rearrange("(i p) r -> p i r", p=P)
        wq_dram = wq.rearrange("(i p) c -> p i c", p=P)
        wk_sb = held.tile([P, CB, C], BF16, name="wk_sb")
        nc.scalar.dma_start(wk_sb[:, :, 0:P], wk_dram[:, :, 0:P])
        wq_sb = held.tile([P, CB, C], BF16, name="wq_sb")
        nc.scalar.dma_start(wq_sb[:, :, 0:P], wq_dram[:, :, 0:P])
        bq_sb = held.tile([P, CB], F32, name="bq_sb")
        nc.scalar.dma_start(bq_sb[:], bq.rearrange("(b p) o -> p (b o)", p=P))
        wv_sb = held.tile([P, CB, C], BF16, name="wv_sb")
        bv_sb = held.tile([P, CB], F32, name="bv_sb")
        wo_sb = held.tile([P, CB, C], BF16, name="wo_sb")
        bo_sb = held.tile([P, CB], F32, name="bo_sb")

        head_sel = held.tile([P, HB], BF16, name="head_sel")
        nc.vector.memset(head_sel[:], 0.0)
        for hd in range(HB):
            nc.vector.memset(head_sel[hd * DK : (hd + 1) * DK, hd : hd + 1], 1.0)
        coef = held.tile([P, KN, KN, KN], BF16, name="coef")
        nc.vector.memset(coef[:], 0.0)
        for a in range(KN):
            nc.vector.memset(coef[:, a, a, :], 1.0)
            nc.vector.memset(coef[:, a, :, a], -1.0)
            nc.vector.memset(coef[:, a, a, a : a + 1], 0.0)
        pair_sel = held.tile([P, KN, PAIRS * HB], BF16, name="pair_sel")
        nc.vector.tensor_tensor(
            pair_sel[:].rearrange("p a (z r) -> p (a z) r", r=HB),
            coef[:].rearrange("p a x y -> p (a x y)").unsqueeze(2).to_broadcast([P, KN * PAIRS, HB]),
            head_sel[:].unsqueeze(1).to_broadcast([P, KN * PAIRS, HB]),
            ALU.mult,
        )
        ident = held.tile([P, P], F32, name="ident")
        make_identity(nc, ident[:])
        ident_bf = held.tile([P, P], BF16, name="ident_bf")
        make_identity(nc, ident_bf[:])

        h_bf = [held.tile([P, CB, BANK], BF16, name=f"h_bf{n}") for n in range(NB)]
        k_sb = {}
        q_sb = {}
        v_sb = [held.tile([P, S], F32, name=f"v_sb{b}") for b in range(CB)]

        def project_chunk(dst, w_sb, bias, b, n):
            acc = psum.tile([P, BANK], F32, name="acc", tag="bank")
            for i in range(CB):
                nc.tensor.matmul(
                    acc[:],
                    w_sb[:, i, b * P : (b + 1) * P],
                    h_bf[n][:, i, :],
                    start=(i == 0),
                    stop=(i == CB - 1),
                )
            cols = slice(n * BANK, (n + 1) * BANK)
            if bias is None:
                nc.scalar.copy(dst[:, cols], acc[:])
            else:
                nc.scalar.activation(dst[:, cols], acc[:], FUNC.Identity, bias=bias[:, b : b + 1])

        def parked(first_block, blocks):
            rows = KN * HB
            first = C - CB * rows + first_block * rows
            return out[first : first + blocks * rows, :].rearrange("x n -> (x n)")

        diffs = {}
        exps = {}
        sums = {}

        def pair_sums(t_bf, b, a):
            if a == 0:
                diffs[b] = [
                    psum.tile([P, PAIRS * HB, BANK_TILES], F32, name="diff", tag="bank")
                    for s in range(TILE_SETS)
                ]
            for k in range(PT):
                nc.tensor.matmul(
                    diffs[b][k % TILE_SETS][:, :, k // TILE_SETS],
                    t_bf[:, k * P : (k + 1) * P],
                    pair_sel[:, a, :],
                    start=(a == 0 and k // TILE_SETS == 0),
                    stop=(a == KN - 1 and k // TILE_SETS == BANK_TILES - 1),
                )

        def softmax_exp(b):
            exps[b] = soft.tile([P, TILE_SETS, BANK], F32, name="e")
            for s in range(TILE_SETS):
                nc.scalar.activation(
                    exps[b][:, s, :],
                    diffs[b][s][:].rearrange("p z k -> p (z k)"),
                    FUNC.Exp,
                    scale=1.0 / math.sqrt(DK),
                )

        def softmax_flip(b):
            if b % GB == 0:
                sums[b // GB] = psum.tile([P, GB, TILE_SETS, P], F32, name="z_rows", tag="bank")
            for s in range(TILE_SETS):
                for x in range(KN):
                    nc.tensor.matmul(
                        sums[b // GB][:, b % GB, s, :],
                        exps[b][:, s, x * P : (x + 1) * P],
                        ident[:],
                        start=(s == 0 and x == 0),
                        stop=(s == TILE_SETS - 1 and x == KN - 1),
                        is_transpose=True,
                    )

        def softmax_park(group):
            ln_z = park.tile([P, GB, TILE_SETS * P], F32, name="ln_z")
            nc.scalar.activation(ln_z[:], sums[group][:].rearrange("p j s w -> p j (s w)"), FUNC.Ln)
            p_rows = park.tile([P, GB, TILE_SETS * P], F32, name="p_rows")
            nc.scalar.activation(p_rows[:], ln_z[:], FUNC.Exp, scale=-1.0)
            nc.sync.dma_start(
                parked(group * GB, GB).rearrange("(j r v) -> r j v", j=GB, v=TILE_SETS * P), p_rows[:]
            )
            parked_blocks.extend(range(group * GB, (group + 1) * GB))
            fetch_p()

        def softmax_after(item):
            b, lag = divmod(item, KN)
            if b >= 1 and lag == 0:
                softmax_exp(b - 1)
            if b >= 1 and lag == 1:
                softmax_flip(b - 1)
            if b >= 1 and lag == 2 and b % GB == 0:
                softmax_park(b // GB - 1)

        steps = [(b, n0, WIDE) for n0 in range(0, S, WIDE) for b in range(GB)]
        for n0 in range(0, S, WIDE):
            steps.extend((b, n0, WIDE) for b in range(GB, CB - 1))
            steps.append((CB - 1, n0, BANK))
            if n0 + WIDE < S:
                steps.append((CB - 1, n0 + BANK, BANK))
            else:
                steps.extend((CB - 1, n0 + BANK + x, BANK // 2) for x in (0, BANK // 2))

        p_full = []
        parked_blocks = []
        spent = []

        def fetch_p():
            while (
                len(p_full) < min(len(spent) + AHEAD, len(steps))
                and steps[len(p_full)][0] in parked_blocks
            ):
                b, n0, width = steps[len(p_full)]
                by_head = parked(b, 1).rearrange("(a r n) -> r a n", a=KN, n=S)
                p_tile = p_ring.tile([P, KN, WIDE], F32, name="p_full")
                for hd in range(HB):
                    queue = nc.sync if hd < HB // 2 else nc.gpsimd
                    queue.dma_start(
                        p_tile[hd * DK : (hd + 1) * DK, :, 0:width],
                        by_head[hd, :, n0 : n0 + width]
                        .unsqueeze(0)
                        .to_broadcast([DK, KN, width]),
                    )
                p_full.append(p_tile)

        v_made = []

        def project_values(count):
            for x in range(len(v_made), len(v_made) + count):
                project_chunk(v_sb[x // NB], wv_sb, bv_sb, x // NB, x % NB)
                v_made.append(x)

        with (
            tc.tile_pool(name="kq_ring", bufs=2) as kq_ring,
            tc.tile_pool(name="t_ring", bufs=2) as t_ring,
        ):
            h_f32 = [p_ring.tile([P, CB, BANK], F32, name="h_f32", tag="p_full") for n in range(NB)]
            for n in range(NB - 1):
                nc.sync.dma_start(
                    h_f32[n][:], h[:, n * BANK : (n + 1) * BANK].rearrange("(i p) n -> p i n", p=P)
                )
            nc.sync.dma_start(offsets[:], offs)
            for i in range(CB):
                nc.sync.dma_start(
                    h_f32[NB - 1][:, i, :], h[i * P : (i + 1) * P, (NB - 1) * BANK : NB * BANK]
                )
            nc.sync.dma_start(wk_sb[:, :, P:C], wk_dram[:, :, P:C])
            nc.sync.dma_start(wv_sb[:], wkv[:, C : 2 * C].rearrange("(i p) r -> p i r", p=P))
            nc.sync.dma_start(bv_sb[:], bv.rearrange("(b p) o -> p (b o)", p=P))
            nc.sync.dma_start(wq_sb[:, :, P:C], wq_dram[:, :, P:C])
            nc.sync.dma_start(wo_sb[:], wo.rearrange("(i p) m -> p i m", p=P))
            nc.sync.dma_start(bo_sb[:], bo.rearrange("(b p) o -> p (b o)", p=P))
            k_sb[0] = kq_ring.tile([P, S], F32, name="k_sb")
            q_sb[0] = kq_ring.tile([P, S], F32, name="q_sb")
            for n in range(NB):
                for i in range(CB):
                    nc.vector.tensor_copy(h_bf[n][:, i, :], h_f32[n][:, i, :])
                project_chunk(k_sb[0], wk_sb, None, 0, n)
                if n < NB // 2:
                    project_chunk(q_sb[0], wq_sb, bq_sb, 0, n)
            for n in range(NB // 2, NB):
                project_chunk(q_sb[0], wq_sb, bq_sb, 0, n)

            def project_beside(item):
                b, a = divmod(item, KN)
                if b + 1 < CB:
                    if a == 0:
                        k_sb[b + 1] = kq_ring.tile([P, S], F32, name="k_sb")
                        q_sb[b + 1] = kq_ring.tile([P, S], F32, name="q_sb")
                    for n in (2 * a % NB, 2 * a % NB + 1):
                        if a < KN // 2:
                            project_chunk(k_sb[b + 1], wk_sb, None, b + 1, n)
                        else:
                            project_chunk(q_sb[b + 1], wq_sb, bq_sb, b + 1, n)
                    if item >= KEY_ITEMS - KN - (CB * NB - 3 * KN):
                        project_values(1)
                else:
                    project_values(3)

            before = None
            project_beside(0)
            for item in range(KEY_ITEMS):
                b, a = divmod(item, KN)
                t_f32 = product_ring.tile([P, S], F32, name="t_f32", tag="product")
                width = S // 2 if item == 0 else S
                for n0 in range(0, S, width):
                    j0 = a * S + n0
                    nc.vector.tensor_tensor(
                        t_f32[:, n0 : n0 + width],
                        k_sb[b][:].indirect(offsets[:, j0 // 16 : (j0 + width) // 16]),
                        q_sb[b][:, n0 : n0 + width],
                        ALU.mult,
                    )
                t_bf = t_ring.tile([P, S], BF16, name="t_bf")
                nc.scalar.copy(t_bf[:], t_f32[:])
                if before is not None:
                    pair_sums(*before)
                before = (t_bf, b, a)
                if item + 1 < KEY_ITEMS:
                    project_beside(item + 1)
                softmax_after(item)
            pair_sums(*before)
            softmax_exp(CB - 1)

        with (
            tc.tile_pool(name="ctx_pool", bufs=1) as ctx_pool,
            tc.tile_pool(name="c_ring", bufs=2) as c_ring,
            tc.tile_pool(name="o_ring", bufs=2 * CB) as o_ring,
        ):
            ctx_bf = [ctx_pool.tile([P, S], BF16, name=f"ctx_bf{b}") for b in range(CB)]
            out_acc = []

            def add_to_out(m, n0, width, blocks):
                for x in blocks:
                    nc.tensor.matmul(
                        out_acc[m][:, 0:width],
                        wo_sb[:, x, m * P : (m + 1) * P],
                        ctx_bf[x][:, n0 : n0 + width],
                        start=(x == 0),
                        stop=(x == CB - 1),
                    )

            for step in range(len(steps)):
                b, n0, width = steps[step]
                if b == CB - 1:
                    out_acc.clear()
                    for m in range(CB):
                        out_acc.append(psum.tile([P, BANK], F32, name="out_acc", tag="bank"))
                        add_to_out(m, n0, width, range(CB - 1))

                u = product_ring.tile([P, KN, WIDE], F32, name="u", tag="product")
                total = u[:, 0, 0:width]
                for a in range(KN):
                    j0 = a * S + n0
                    nc.vector.tensor_tensor(
                        u[:, a, 0:width],
                        v_sb[b][:].indirect(offsets[:, j0 // 16 : (j0 + width) // 16]),
                        p_full[step][:, a, 0:width],
                        ALU.mult,
                    )
                    if step >= len(steps) - VECTOR_SUMS and a > 0:
                        if a < KN - 1:
                            part = c_ring.tile([P, BANK], F32, name="part")
                            new_total = part[:, 0:width]
                        else:
                            new_total = ctx_bf[b][:, n0 : n0 + width]
                        nc.vector.tensor_add(new_total, total, u[:, a, 0:width])
                        total = new_total
                spent.append(step)
                fetch_p()

                if step < len(steps) - VECTOR_SUMS:
                    piece = min(width, BANK)
                    chunks = range(width // piece)
                    ctx_t = [psum.tile([P, BANK // P, P], F32, name="ctx_t", tag="bank") for c in chunks]
                    squares = piece // P
                    for a in range(KN):
                        for c in chunks:
                            for x in range(squares):
                                first = c * piece + x * P
                                nc.tensor.matmul(
                                    ctx_t[c][:, x, :],
                                    u[:, a, first : first + P],
                                    ident[:],
                                    start=(a == 0 and x == 0),
                                    stop=(a == KN - 1 and x == squares - 1),
                                    is_transpose=True,
                                )
                    if step == 0:
                        softmax_flip(CB - 1)
                    for c in chunks:
                        ctx_t_bf = c_ring.tile([P, BANK // P, P], BF16, name="ctx_t_bf")
                        nc.scalar.copy(ctx_t_bf[:, 0:squares, :], ctx_t[c][:, 0:squares, :])
                        ctx_ps = psum.tile([P, BANK], BF16, name="ctx_ps", tag="bank")
                        for x in range(squares):
                            nc.tensor.transpose(
                                ctx_ps[:, x * P : (x + 1) * P], ctx_t_bf[:, x, :], ident_bf[:]
                            )
                        nc.scalar.copy(
                            ctx_bf[b][:, n0 + c * piece : n0 + (c + 1) * piece], ctx_ps[:, 0:piece]
                        )
                    if step == 0:
                        softmax_park(CB // GB - 1)

                if b == CB - 1:
                    for m in range(CB):
                        add_to_out(m, n0, width, [CB - 1])
                        o = o_ring.tile([P, BANK], F32, name="o")
                        if step == len(steps) - 1 and m % 2 == 1:
                            nc.vector.tensor_scalar_add(
                                o[:, 0:width], out_acc[m][:, 0:width], bo_sb[:, m : m + 1]
                            )
                        else:
                            nc.scalar.activation(
                                o[:, 0:width],
                                out_acc[m][:, 0:width],
                                FUNC.Identity,
                                bias=bo_sb[:, m : m + 1],
                            )
                        nc.sync.dma_start(out[m * P : (m + 1) * P, n0 : n0 + width], o[:, 0:width])
